import numpy as np
import ml_dtypes


def mxq(x, axis, fmt="e4m3"):
    dtype, down = {"e4m3": (ml_dtypes.float8_e4m3fn, 7), "e5m2": (ml_dtypes.float8_e5m2, 14)}[fmt]
    v = np.moveaxis(np.asarray(x, np.float32).astype(ml_dtypes.bfloat16).astype(np.float64), axis, -1)
    blocks = v.reshape(v.shape[:-1] + (-1, 32))
    amax = np.abs(blocks).max(-1, keepdims=True)
    byte = np.maximum(np.where(amax > 0, np.frexp(amax)[1] - 1 + 127, 0) - down, 1)
    scale = np.exp2(byte - 127.0)
    codes = (blocks / scale).astype(np.float32).astype(dtype).astype(np.float64)
    return np.moveaxis((codes * scale).reshape(v.shape), -1, axis)


WIDE = False


def mx_kscale(k):
    if not WIDE:
        return np.ones(k)
    levels = np.array([10, -10, 5, -5, 0])
    a = np.random.permutation(np.resize(levels, k // 512 * 4)).reshape(k // 512, 4)
    idx = np.arange(k)
    return np.exp2(a[idx // 512, idx % 128 // 32])


BF16 = ml_dtypes.bfloat16


def bf(x):
    return np.asarray(x, np.float32).astype(BF16)


def f64(x):
    return np.asarray(x).astype(np.float64)


N, D, L = 1024, 1024, 4
EPS = 1e-5
SLOPE = 0.1


def leaky(v):
    return np.where(v >= 0, v, SLOPE * v)


def layernorm(h, g, b):
    mu = np.mean(h, axis=-1, keepdims=True)
    var = np.mean((h - mu) ** 2, axis=-1, keepdims=True)
    return (h - mu) * (1.0 / np.sqrt(var + EPS)) * g + b


def setup_inputs():
    s, t = mx_kscale(N), mx_kscale(D)
    g = np.random.standard_normal((N, N))
    sq = (g * g.T) ** 2
    lap = 0.5 * (sq / sq.sum(axis=1, keepdims=True) + np.eye(N))
    feat = leaky(np.random.standard_normal((N, D)))
    return {"lap": bf(lap * s[None, :]),
            "feat": bf(feat / s[:, None] * t[None, :]),
            "w": bf(np.random.standard_normal((D, D)) / np.sqrt(D) / t[None, :]),
            "gamma": bf(1.0 + 0.1 * np.random.standard_normal(D)),
            "beta": bf(0.1 * np.random.standard_normal(D))}


def reference(lap, feat, w, gamma, beta):
    m = mxq(f64(lap), 1, "e4m3") @ mxq(f64(feat), 0, "e4m3")
    y = mxq(m, 1, "e4m3") @ mxq(f64(w), 1, "e4m3").T
    return leaky(layernorm(y, f64(gamma), f64(beta)))

@@ -1,0 +1,471 @@
+from contextlib import ExitStack
+
+import concourse.mybir as mybir
+from concourse.masks import make_identity
+
+F32 = mybir.dt.float32
+BF16 = mybir.dt.bfloat16
+U32 = mybir.dt.uint32
+U8 = mybir.dt.uint8
+FP8X4 = mybir.dt.float8_e4m3fn_x4
+ALU = mybir.AluOpType
+ACT = mybir.ActivationFunctionType
+
+P = 128
+N = 1024
+D = 1024
+NT = N // P
+EPS = 1e-5
+SLOPE = 0.1
+FLOPS = 2 * 2 * N * N * D
+MANUAL = True
+
+ORDER = (
+    ("GBp", (0,), "PE"),
+    ("GBp", (1,), "PE"),
+    ("RG", (0, 0, 0,), "V"),
+    ("RG", (0, 1, 0,), "S"),
+    ("RG", (0, 0, 1,), "V"),
+    ("RG", (0, 1, 1,), "S"),
+    ("FQ", (0, 0,), "V"),
+    ("RG", (1, 0, 0,), "V"),
+    ("RG", (1, 1, 1,), "S"),
+    ("RG", (1, 0, 1,), "V"),
+    ("Lp", (0,), "PE"),
+    ("RG", (1, 1, 0,), "V"),
+    ("Lp", (1,), "PE"),
+    ("Ls", (0,), "S"),
+    ("FQ", (0, 1,), "V"),
+    ("Ls", (1,), "S"),
+    ("Wp", (0, 0,), "PE"),
+    ("FQ", (1, 0,), "V"),
+    ("Ws", (0, 0,), "S"),
+    ("Wp", (0, 1,), "PE"),
+    ("FQ", (1, 1,), "V"),
+    ("Ws", (0, 1,), "S"),
+    ("Wp", (1, 0,), "PE"),
+    ("Lv", (0,), "V"),
+    ("Lv", (1,), "V"),
+    ("Ws", (1, 0,), "S"),
+    ("Wp", (1, 1,), "PE"),
+    ("M1p", (0, 0,), "PE"),
+    ("Ws", (1, 1,), "V"),
+    ("Wp", (2, 0,), "PE"),
+    ("Wv", (0, 0,), "V"),
+    ("M1s", (0, 0,), "S"),
+    ("Wp", (2, 1,), "PE"),
+    ("Wv", (0, 1,), "V"),
+    ("Ws", (2, 0,), "S"),
+    ("M1p", (0, 1,), "PE"),
+    ("Ws", (2, 1,), "V"),
+    ("Wp", (3, 0,), "PE"),
+    ("M1s", (0, 1,), "S"),
+    ("Wp", (3, 1,), "PE"),
+    ("Ws", (3, 0,), "V"),
+    ("M1p", (1, 0,), "PE"),
+    ("Ws", (3, 1,), "S"),
+    ("Wv", (1, 0,), "V"),
+    ("M1p", (1, 1,), "PE"),
+    ("M1s", (1, 0,), "S"),
+    ("M1v", (0,), "V"),
+    ("Wv", (1, 1,), "V"),
+    ("Lp", (2,), "PE"),
+    ("M1s", (1, 1,), "S"),
+    ("Lp", (3,), "PE"),
+    ("Ls", (2,), "V"),
+    ("M2p", (0, 0,), "PE"),
+    ("Ls", (3,), "S"),
+    ("M1v", (1,), "V"),
+    ("M2p", (0, 1,), "PE"),
+    ("Lv", (2,), "V"),
+    ("S1", (0, 0,), "S"),
+    ("Lv", (3,), "V"),
+    ("Lp", (4,), "PE"),
+    ("S1", (0, 1,), "S"),
+    ("M1p", (2, 0,), "PE"),
+    ("Ls", (4,), "V"),
+    ("M1p", (2, 1,), "PE"),
+    ("NM", (0,), "V"),
+    ("A", (0,), "V"),
+    ("M1s", (2, 0,), "S"),
+    ("M2p", (1, 0,), "PE"),
+    ("S2", (0,), "S"),
+    ("M1p", (3, 0,), "PE"),
+    ("M1s", (2, 1,), "V"),
+    ("M2p", (1, 1,), "PE"),
+    ("M1v", (2,), "V"),
+    ("M1s", (3, 0,), "S"),
+    ("Lv", (4,), "V"),
+    ("M1p", (3, 1,), "PE"),
+    ("SQ", (0,), "S"),
+    ("S1", (1, 0,), "S"),
+    ("RC", (0,), "V"),
+    ("M1p", (4, 0,), "PE"),
+    ("B", (0,), "V"),
+    ("M1s", (3, 1,), "S"),
+    ("Lp", (5,), "PE"),
+    ("M1s", (4, 0,), "S"),
+    ("M2p", (2, 0,), "PE"),
+    ("M1v", (3,), "V"),
+    ("C", (0,), "V"),
+    ("S1", (1, 1,), "S"),
+    ("M1p", (4, 1,), "PE"),
+    ("Ls", (5,), "S"),
+    ("Lp", (6,), "PE"),
+    ("M1s", (4, 1,), "V"),
+    ("M2p", (2, 1,), "PE"),
+    ("S1", (2, 0,), "S"),
+    ("M1v", (4,), "V"),
+    ("Ls", (6,), "S"),
+    ("Lp", (7,), "PE"),
+    ("NM", (1,), "V"),
+    ("A", (1,), "V"),
+    ("M2p", (3, 0,), "PE"),
+    ("S2", (1,), "S"),
+    ("Lv", (5,), "V"),
+    ("Lv", (6,), "V"),
+    ("SQ", (1,), "S"),
+    ("M1p", (5, 0,), "PE"),
+    ("S1", (2, 1,), "S"),
+    ("RC", (1,), "V"),
+    ("B", (1,), "V"),
+    ("M1p", (5, 1,), "PE"),
+    ("S1", (3, 0,), "S"),
+    ("M2p", (3, 1,), "PE"),
+    ("M1s", (5, 0,), "S"),
+    ("NM", (2,), "V"),
+    ("A", (2,), "V"),
+    ("M2p", (4, 0,), "PE"),
+    ("M1s", (5, 1,), "S"),
+    ("M1p", (6, 0,), "PE"),
+    ("S2", (2,), "S"),
+    ("M1v", (5,), "V"),
+    ("C", (1,), "V"),
+    ("M1p", (6, 1,), "PE"),
+    ("SQ", (2,), "S"),
+    ("M1s", (6, 0,), "S"),
+    ("RC", (2,), "V"),
+    ("B", (2,), "V"),
+    ("M1s", (6, 1,), "S"),
+    ("S1", (3, 1,), "S"),
+    ("M1v", (6,), "V"),
+    ("C", (2,), "V"),
+    ("Ls", (7,), "S"),
+    ("M2p", (4, 1,), "PE"),
+    ("S1", (4, 0,), "S"),
+    ("NM", (3,), "V"),
+    ("A", (3,), "V"),
+    ("S1", (4, 1,), "S"),
+    ("M2p", (5, 0,), "PE"),
+    ("S2", (3,), "S"),
+    ("M2p", (5, 1,), "PE"),
+    ("Lv", (7,), "V"),
+    ("NM", (4,), "V"),
+    ("A", (4,), "V"),
+    ("M1p", (7, 0,), "PE"),
+    ("SQ", (3,), "S"),
+    ("S2", (4,), "S"),
+    ("M1p", (7, 1,), "PE"),
+    ("RC", (3,), "V"),
+    ("B", (3,), "V"),
+    ("M1s", (7, 0,), "S"),
+    ("C", (3,), "V"),
+    ("M1s", (7, 1,), "S"),
+    ("SQ", (4,), "S"),
+    ("S1", (5, 0,), "S"),
+    ("M1v", (7,), "V"),
+    ("RC", (4,), "V"),
+    ("B", (4,), "V"),
+    ("S1", (5, 1,), "S"),
+    ("M2p", (6, 0,), "PE"),
+    ("M2p", (6, 1,), "PE"),
+    ("S1", (6, 0,), "S"),
+    ("NM", (5,), "V"),
+    ("A", (5,), "V"),
+    ("S2", (5,), "S"),
+    ("M2p", (7, 0,), "PE"),
+    ("C", (4,), "V"),
+    ("SQ", (5,), "S"),
+    ("S1", (6, 1,), "S"),
+    ("RC", (5,), "V"),
+    ("B", (5,), "V"),
+    ("S1", (7, 0,), "S"),
+    ("M2p", (7, 1,), "PE"),
+    ("S1", (7, 1,), "S"),
+    ("NM", (6,), "V"),
+    ("A", (6,), "V"),
+    ("S2", (6,), "S"),
+    ("C", (5,), "V"),
+    ("SQ", (6,), "S"),
+    ("NM", (7,), "V"),
+    ("A", (7,), "V"),
+    ("S2", (7,), "S"),
+    ("RC", (6,), "V"),
+    ("B", (6,), "V"),
+    ("SQ", (7,), "S"),
+    ("C", (6,), "V"),
+    ("RC", (7,), "V"),
+    ("B", (7,), "V"),
+    ("C", (7,), "V"),
+)
+
+
+def tile_gcn_pb_kernel(tc, lap, feat, w, gamma, beta, out):
+    nc = tc.nc
+    with ExitStack() as ctx:
+        keep = ctx.enter_context(tc.tile_pool(name="keep", bufs=1))
+        ypool = ctx.enter_context(tc.tile_pool(name="ypool", bufs=4))
+        opool = ctx.enter_context(tc.tile_pool(name="opool", bufs=4))
+        small = ctx.enter_context(tc.tile_pool(name="small", bufs=6))
+        psum = ctx.enter_context(tc.psum_pool(name="psum", bufs=2))
+        if MANUAL:
+            ctx.enter_context(tc.manual_schedule())
+
+        eps_t = keep.tile([P, 1], F32)
+        nc.vector.memset(eps_t[:], EPS)
+        warm = keep.tile([P, 1], F32)
+        nc.scalar.activation(out=warm[:], in_=eps_t[:], func=ACT.Sqrt)
+        ident = keep.tile([P, P], F32)
+        make_identity(nc, ident[:])
+        ones = keep.tile([P, P], BF16)
+        nc.vector.memset(ones[:], 1.0)
+        gb_row = keep.tile([P, 2 * D], BF16)
+        nc.vector.memset(gb_row[:], 0.0)
+        nc.sync.dma_start(out=gb_row[0:1, 0:D], in_=gamma.rearrange("(o d) -> o d", o=1))
+        nc.sync.dma_start(out=gb_row[0:1, D : 2 * D], in_=beta.rearrange("(o d) -> o d", o=1))
+
+        fr = keep.tile([P, 2, 4, D], BF16)
+        lap_sb = keep.tile([P, NT, N], BF16)
+        w_sb = keep.tile([P, NT, D], BF16)
+        lap_v = lap.rearrange("(p t) j -> p t j", t=NT)
+
+        def load_w():
+            for k in range(4):
+                nc.sync.dma_start(
+                    out=w_sb[:, 2 * k : 2 * k + 2, :],
+                    in_=w[256 * k : 256 * k + 256, :].rearrange("(t p) d -> p t d", p=P),
+                )
+
+        for g in range(2):
+            for u in range(2):
+                r0 = 512 * g + 256 * u
+                nc.sync.dma_start(
+                    out=fr[:, g, 2 * u : 2 * u + 2, :],
+                    in_=feat[r0 : r0 + 256, :].rearrange("(q e) c -> q e c", e=2),
+                )
+        nc.sync.dma_start(out=lap_sb[:, 0:2, :], in_=lap_v[:, 0:2, :])
+        load_w()
+        nc.sync.dma_start(out=lap_sb[:, 2:4, :], in_=lap_v[:, 2:4, :])
+        nc.sync.dma_start(out=lap_sb[:, 4:8, :], in_=lap_v[:, 4:8, :])
+        lap_w = lap_sb[:].bitcast(F32)
+        w_w = w_sb[:].bitcast(F32)
+
+        fg = keep.tile([P, 2, D, 4], BF16, align_bytes=64)
+        f_codes = keep.tile([P, 2, D], U32, align_bytes=64)
+        f_sc = keep.tile([P, 2, D], U8, align_bytes=64)
+        lg = keep.tile([P, NT, 2, P, 4], BF16, align_bytes=64)
+        lg_w = lg[:].bitcast(F32)
+        l_codes = keep.tile([P, NT, 2, P], U32, align_bytes=64)
+        l_sc = keep.tile([P, NT, 2, P], U8, align_bytes=64)
+        wg = keep.tile([P, 2, D, 4], BF16, align_bytes=64)
+        wg_w = wg[:].bitcast(F32)
+        w_codes = keep.tile([P, 2, D], U32, align_bytes=64)
+        w_sc = keep.tile([P, 2, D], U8, align_bytes=64)
+        mg = keep.tile([P, NT, 2, P, 4], BF16, align_bytes=64)
+        m_codes = keep.tile([P, NT, 2, P], U32, align_bytes=64)
+        m_sc = keep.tile([P, NT, 2, P], U8, align_bytes=64)
+        junk = keep.tile([P, D], BF16)
+        out_v = out.rearrange("(p t) o -> p t o", t=NT)
+        live = {}
+
+        def copy_on(eng, dst, src):
+            if eng == "V":
+                nc.vector.tensor_copy(out=dst, in_=src)
+            else:
+                nc.scalar.copy(out=dst, in_=src)
+
+        def op_GBp(a, eng):
+            k = a[0]
+            bank = psum.tile([P, D], BF16, name="gb%d" % k, tag="gb%d" % k, bufs=1)
+            for h in range(2):
+                c0 = D * k + 512 * h
+                nc.tensor.matmul(
+                    out=bank[:, 512 * h : 512 * h + 512], lhsT=ones[:], rhs=gb_row[:, c0 : c0 + 512], start=True, stop=True
+                )
+            live[("gb", k)] = bank
+
+        def op_RG(a, eng):
+            g, g2, u = a
+            c0 = 512 * g2 + 256 * u
+            src = fr[:, g, :, c0 : c0 + 256].rearrange("p t (c i e) -> p e c t i", i=4, e=2)
+            dst = fg[:, g, c0 : c0 + 256, :].rearrange("p (e c i) t -> p e c t i", e=2, i=4)
+            if eng == "V":
+                nc.vector.tensor_copy(out=dst, in_=src)
+            else:
+                for e in range(2):
+                    nc.scalar.copy(out=dst[:, e], in_=src[:, e])
+
+        def op_FQ(a, eng):
+            g, g2 = a
+            cs = slice(512 * g2, 512 * g2 + 512)
+            nc.vector.quantize_mx(
+                out=f_codes[:, g, cs].bitcast(FP8X4),
+                scales=f_sc[:, g, cs],
+                in_=fg[:, g, cs, :].rearrange("p c t -> p (c t)"),
+            )
+
+        def op_Lp(a, eng):
+            it = a[0]
+            tp = psum.tile([P, 2, 2, P], F32, name="tp", tag="tp", bufs=2)
+            for g in range(2):
+                for u in range(2):
+                    c0 = 256 * g + 128 * u
+                    nc.tensor.transpose(tp[:, g, u, :], lap_w[:, it, c0 : c0 + 128], ident[:])
+            live[("L", it)] = tp
+
+        def op_Ls(a, eng):
+            it = a[0]
+            copy_on(eng, lg_w[:, it], live[("L", it)][:].rearrange("p g u i -> p g i u"))
+
+        def op_Lv(a, eng):
+            it = a[0]
+            nc.vector.quantize_mx(
+                out=l_codes[:, it].rearrange("p g i -> p (g i)").bitcast(FP8X4),
+                scales=l_sc[:, it].rearrange("p g i -> p (g i)"),
+                in_=lg[:, it].rearrange("p g i t -> p (g i t)"),
+            )
+
+        def op_Wp(a, eng):
+            pr, g2 = a
+            tp = psum.tile([P, 2, 2, P], F32, name="tp", tag="tp", bufs=2)
+            for b in range(2):
+                for u in range(2):
+                    c0 = 256 * g2 + 128 * u
+                    nc.tensor.transpose(tp[:, u, b, :], w_w[:, 2 * pr + b, c0 : c0 + 128], ident[:])
+            live[("W", pr, g2)] = tp
+
+        def op_Ws(a, eng):
+            pr, g2 = a
+            copy_on(eng, wg_w[:, g2, 256 * pr : 256 * pr + 256, :], live[("W", pr, g2)][:].rearrange("p u b o -> p (b o) u"))
+
+        def op_Wv(a, eng):
+            h, g2 = a
+            cs = slice(512 * h, 512 * h + 512)
+            nc.vector.quantize_mx(
+                out=w_codes[:, g2, cs].bitcast(FP8X4),
+                scales=w_sc[:, g2, cs],
+                in_=wg[:, g2, cs, :].rearrange("p c t -> p (c t)"),
+            )
+
+        def op_M1p(a, eng):
+            it, g2 = a
+            mp = psum.tile([P, 4, P], F32, name="mp", tag="mp", bufs=2)
+            for t2 in range(4):
+                cs = slice((4 * g2 + t2) * P, (4 * g2 + t2 + 1) * P)
+                for g in range(2):
+                    nc.tensor.matmul_mx(
+                        out=mp[:, t2, :],
+                        lhsT=f_codes[:, g, cs].bitcast(FP8X4),
+                        lhsT_scale=f_sc[:, g, cs],
+                        rhs=l_codes[:, it, g, :].bitcast(FP8X4),
+                        rhs_scale=l_sc[:, it, g, :],
+                        start=(g == 0),
+                        stop=(g == 1),
+                    )
+            live[("M", it, g2)] = mp
+
+        def op_M1s(a, eng):
+            it, g2 = a
+            copy_on(eng, mg[:, it, g2], live[("M", it, g2)][:].rearrange("p t i -> p i t"))
+
+        def op_M1v(a, eng):
+            it = a[0]
+            nc.vector.quantize_mx(
+                out=m_codes[:, it].rearrange("p g i -> p (g i)").bitcast(FP8X4),
+                scales=m_sc[:, it].rearrange("p g i -> p (g i)"),
+                in_=mg[:, it].rearrange("p g i t -> p (g i t)"),
+            )
+
+        def op_M2p(a, eng):
+            it, h = a
+            yp = psum.tile([P, 512], F32, name="yp", tag="yp", bufs=2)
+            cs = slice(512 * h, 512 * h + 512)
+            for g2 in range(2):
+                nc.tensor.matmul_mx(
+                    out=yp[:],
+                    lhsT=m_codes[:, it, g2, :].bitcast(FP8X4),
+                    lhsT_scale=m_sc[:, it, g2, :],
+                    rhs=w_codes[:, g2, cs].bitcast(FP8X4),
+                    rhs_scale=w_sc[:, g2, cs],
+                    start=(g2 == 0),
+                    stop=(g2 == 1),
+                )
+            live[("Y", it, h)] = yp
+
+        def op_S1(a, eng):
+            it, h = a
+            if h == 0:
+                live[("ysb", it)] = ypool.tile([P, D], F32, name="y_sb", tag="y_sb")
+                live[("sums", it)] = small.tile([P, 2], F32, name="sums", tag="sums")
+            cs = slice(512 * h, 512 * h + 512)
+            nc.scalar.activation(
+                out=live[("ysb", it)][:, cs], in_=live[("Y", it, h)][:], func=ACT.Copy, accum_out=live[("sums", it)][:, h : h + 1]
+            )
+
+        def op_NM(a, eng):
+            it = a[0]
+            negmu = small.tile([P, 1], F32, name="negmu", tag="negmu")
+            sums = live[("sums", it)]
+            nc.vector.tensor_scalar(
+                out=negmu[:], in0=sums[:, 0:1], scalar1=sums[:, 1:2], scalar2=-1.0 / D, op0=ALU.add, op1=ALU.mult
+            )
+            live[("negmu", it)] = negmu
+
+        def op_S2(a, eng):
+            it = a[0]
+            ssq = small.tile([P, 1], F32, name="ssq", tag="ssq")
+            nc.scalar.activation(
+                out=junk[:], in_=live[("ysb", it)][:], func=ACT.Square, bias=live[("negmu", it)][:, 0:1], scale=1.0, accum_out=ssq[:]
+            )
+            live[("ssq", it)] = ssq
+
+        def op_SQ(a, eng):
+            it = a[0]
+            std = small.tile([P, 1], F32, name="std", tag="std")
+            nc.scalar.activation(out=std[:], in_=live[("ssq", it)][:], func=ACT.Sqrt, bias=eps_t[:, 0:1], scale=1.0 / D)
+            live[("std", it)] = std
+
+        def op_RC(a, eng):
+            it = a[0]
+            rstd = small.tile([P, 1], F32, name="rstd", tag="rstd")
+            nc.vector.reciprocal(out=rstd[:], in_=live[("std", it)][:])
+            live[("rstd", it)] = rstd
+
+        def op_A(a, eng):
+            it = a[0]
+            z = opool.tile([P, D], F32, name="z", tag="z")
+            nc.vector.scalar_tensor_tensor(
+                out=z[:], in0=live[("ysb", it)][:], scalar=live[("negmu", it)][:, 0:1], in1=live[("gb", 0)][:], op0=ALU.add, op1=ALU.mult
+            )
+            live[("z", it)] = z
+
+        def op_B(a, eng):
+            it = a[0]
+            z = live[("z", it)]
+            nc.vector.scalar_tensor_tensor(
+                out=z[:], in0=z[:], scalar=live[("rstd", it)][:, 0:1], in1=live[("gb", 1)][:], op0=ALU.mult, op1=ALU.add
+            )
+
+        def op_C(a, eng):
+            it = a[0]
+            z = live[("z", it)]
+            nc.vector.scalar_tensor_tensor(out=z[:], in0=z[:], scalar=SLOPE, in1=z[:], op0=ALU.mult, op1=ALU.max)
+            nc.sync.dma_start(out=out_v[:, it, :], in_=z[:])
+
+        table = {
+            "GBp": op_GBp, "RG": op_RG, "FQ": op_FQ, "Lp": op_Lp, "Ls": op_Ls, "Lv": op_Lv, "Wp": op_Wp, "Ws": op_Ws,
+            "Wv": op_Wv, "M1p": op_M1p, "M1s": op_M1s, "M1v": op_M1v, "M2p": op_M2p, "S1": op_S1, "NM": op_NM,
+            "S2": op_S2, "SQ": op_SQ, "RC": op_RC, "A": op_A, "B": op_B, "C": op_C,
+        }
+        for kind, args, eng in ORDER:
+            table[kind](args, eng)

@@ -19,194 +19,188 @@ EPS = 1e-5
 SLOPE = 0.1
 FLOPS = 2 * 2 * N * N * D
 MANUAL = True
+LAST_TILE = 6
+LAST_PIECES = 2
 
 ORDER = (
-    ("GBp", (0,), "PE"),
-    ("GBp", (1,), "PE"),
-    ("RG", (0, 0, 0,), "V"),
-    ("RG", (0, 1, 0,), "S"),
-    ("RG", (0, 0, 1,), "V"),
-    ("RG", (0, 1, 1,), "S"),
-    ("FQ", (0, 0,), "V"),
-    ("RG", (1, 0, 0,), "V"),
-    ("RG", (1, 1, 1,), "S"),
-    ("RG", (1, 0, 1,), "V"),
-    ("Lp", (0,), "PE"),
-    ("RG", (1, 1, 0,), "V"),
+    ("RG", (0, 1, 0,), "V"),
+    ("RG", (0, 0, 0,), "S"),
+    ("RG", (0, 1, 1,), "V"),
     ("Lp", (1,), "PE"),
-    ("Ls", (0,), "S"),
+    ("RG", (0, 0, 1,), "S"),
     ("FQ", (0, 1,), "V"),
+    ("Lp", (0,), "PE"),
     ("Ls", (1,), "S"),
+    ("FQ", (0, 0,), "V"),
+    ("Ls", (0,), "S"),
+    ("Lv", (1,), "V"),
+    ("RG", (1, 0, 1,), "S"),
+    ("RG", (1, 0, 0,), "V"),
+    ("RG", (1, 1, 0,), "V"),
     ("Wp", (0, 0,), "PE"),
-    ("FQ", (1, 0,), "V"),
-    ("Ws", (0, 0,), "S"),
     ("Wp", (0, 1,), "PE"),
-    ("FQ", (1, 1,), "V"),
+    ("RG", (1, 1, 1,), "V"),
+    ("Ws", (0, 0,), "S"),
+    ("GBp", (0,), "PE"),
+    ("FQ", (1, 0,), "V"),
     ("Ws", (0, 1,), "S"),
+    ("GBp", (1,), "PE"),
+    ("FQ", (1, 1,), "V"),
     ("Wp", (1, 0,), "PE"),
     ("Lv", (0,), "V"),
-    ("Lv", (1,), "V"),
-    ("Ws", (1, 0,), "S"),
     ("Wp", (1, 1,), "PE"),
-    ("M1p", (0, 0,), "PE"),
-    ("Ws", (1, 1,), "V"),
+    ("Ws", (1, 0,), "S"),
     ("Wp", (2, 0,), "PE"),
-    ("Wv", (0, 0,), "V"),
-    ("M1s", (0, 0,), "S"),
-    ("Wp", (2, 1,), "PE"),
-    ("Wv", (0, 1,), "V"),
-    ("Ws", (2, 0,), "S"),
-    ("M1p", (0, 1,), "PE"),
-    ("Ws", (2, 1,), "V"),
-    ("Wp", (3, 0,), "PE"),
-    ("M1s", (0, 1,), "S"),
-    ("Wp", (3, 1,), "PE"),
-    ("Ws", (3, 0,), "V"),
+    ("Ws", (1, 1,), "S"),
     ("M1p", (1, 0,), "PE"),
-    ("Ws", (3, 1,), "S"),
-    ("Wv", (1, 0,), "V"),
+    ("Wv", (0, 0,), "V"),
+    ("Ws", (2, 0,), "S"),
     ("M1p", (1, 1,), "PE"),
+    ("Wv", (0, 1,), "V"),
     ("M1s", (1, 0,), "S"),
-    ("M1v", (0,), "V"),
-    ("Wv", (1, 1,), "V"),
-    ("Lp", (2,), "PE"),
-    ("M1s", (1, 1,), "S"),
-    ("Lp", (3,), "PE"),
-    ("Ls", (2,), "V"),
-    ("M2p", (0, 0,), "PE"),
-    ("Ls", (3,), "S"),
+    ("Wp", (2, 1,), "PE"),
+    ("M1s", (1, 1,), "V"),
+    ("Wp", (3, 0,), "PE"),
+    ("Ws", (2, 1,), "S"),
+    ("Wp", (3, 1,), "PE"),
     ("M1v", (1,), "V"),
-    ("M2p", (0, 1,), "PE"),
-    ("Lv", (2,), "V"),
-    ("S1", (0, 0,), "S"),
-    ("Lv", (3,), "V"),
-    ("Lp", (4,), "PE"),
-    ("S1", (0, 1,), "S"),
-    ("M1p", (2, 0,), "PE"),
-    ("Ls", (4,), "V"),
-    ("M1p", (2, 1,), "PE"),
-    ("NM", (0,), "V"),
-    ("A", (0,), "V"),
-    ("M1s", (2, 0,), "S"),
+    ("Ws", (3, 0,), "S"),
+    ("Lp", (3,), "PE"),
+    ("Ws", (3, 1,), "V"),
+    ("Lp", (2,), "PE"),
+    ("Wv", (1, 0,), "V"),
+    ("M1p", (0, 0,), "PE"),
+    ("Wv", (1, 1,), "V"),
+    ("Ls", (2,), "S"),
+    ("M1p", (0, 1,), "PE"),
+    ("Ls", (3,), "V"),
+    ("M1s", (0, 0,), "S"),
     ("M2p", (1, 0,), "PE"),
-    ("S2", (0,), "S"),
-    ("M1p", (3, 0,), "PE"),
-    ("M1s", (2, 1,), "V"),
+    ("M1s", (0, 1,), "S"),
+    ("Lv", (2,), "V"),
     ("M2p", (1, 1,), "PE"),
-    ("M1v", (2,), "V"),
-    ("M1s", (3, 0,), "S"),
-    ("Lv", (4,), "V"),
-    ("M1p", (3, 1,), "PE"),
-    ("SQ", (0,), "S"),
+    ("Lv", (3,), "V"),
     ("S1", (1, 0,), "S"),
-    ("RC", (0,), "V"),
-    ("M1p", (4, 0,), "PE"),
-    ("B", (0,), "V"),
-    ("M1s", (3, 1,), "S"),
-    ("Lp", (5,), "PE"),
-    ("M1s", (4, 0,), "S"),
-    ("M2p", (2, 0,), "PE"),
-    ("M1v", (3,), "V"),
-    ("C", (0,), "V"),
+    ("Lp", (4,), "PE"),
+    ("M1v", (0,), "V"),
     ("S1", (1, 1,), "S"),
+    ("M1p", (3, 0,), "PE"),
+    ("Ls", (4,), "S"),
+    ("M1p", (3, 1,), "PE"),
+    ("NM", (1,), "V"),
+    ("M1s", (3, 0,), "V"),
+    ("M1p", (2, 0,), "PE"),
+    ("S2", (1,), "S"),
+    ("Lv", (4,), "V"),
+    ("M1p", (2, 1,), "PE"),
+    ("A", (1,), "V"),
+    ("M2p", (0, 0,), "PE"),
+    ("M1s", (3, 1,), "S"),
+    ("M2p", (0, 1,), "PE"),
+    ("M1s", (2, 0,), "V"),
+    ("SQ", (1,), "S"),
+    ("M1p", (4, 0,), "PE"),
+    ("S1", (0, 0,), "S"),
+    ("M1v", (3,), "V"),
+    ("M1s", (2, 1,), "V"),
     ("M1p", (4, 1,), "PE"),
+    ("S1", (0, 1,), "S"),
+    ("Lp", (5,), "PE"),
+    ("B", (1,), "V"),
+    ("M1s", (4, 0,), "S"),
+    ("M2p", (3, 0,), "PE"),
+    ("M1s", (4, 1,), "S"),
+    ("M1v", (2,), "V"),
+    ("M2p", (3, 1,), "PE"),
     ("Ls", (5,), "S"),
+    ("NM", (0,), "V"),
+    ("C", (1,), "V"),
     ("Lp", (6,), "PE"),
-    ("M1s", (4, 1,), "V"),
+    ("S1", (3, 0,), "S"),
+    ("M2p", (2, 0,), "PE"),
+    ("S2", (0,), "S"),
+    ("A", (0,), "V"),
     ("M2p", (2, 1,), "PE"),
+    ("Lp", (7,), "PE"),
     ("S1", (2, 0,), "S"),
     ("M1v", (4,), "V"),
-    ("Ls", (6,), "S"),
-    ("Lp", (7,), "PE"),
-    ("NM", (1,), "V"),
-    ("A", (1,), "V"),
-    ("M2p", (3, 0,), "PE"),
-    ("S2", (1,), "S"),
     ("Lv", (5,), "V"),
-    ("Lv", (6,), "V"),
-    ("SQ", (1,), "S"),
-    ("M1p", (5, 0,), "PE"),
+    ("SQ", (0,), "S"),
+    ("Ls", (7,), "V"),
     ("S1", (2, 1,), "S"),
-    ("RC", (1,), "V"),
-    ("B", (1,), "V"),
-    ("M1p", (5, 1,), "PE"),
-    ("S1", (3, 0,), "S"),
-    ("M2p", (3, 1,), "PE"),
-    ("M1s", (5, 0,), "S"),
-    ("NM", (2,), "V"),
-    ("A", (2,), "V"),
     ("M2p", (4, 0,), "PE"),
-    ("M1s", (5, 1,), "S"),
-    ("M1p", (6, 0,), "PE"),
-    ("S2", (2,), "S"),
-    ("M1v", (5,), "V"),
-    ("C", (1,), "V"),
-    ("M1p", (6, 1,), "PE"),
-    ("SQ", (2,), "S"),
-    ("M1s", (6, 0,), "S"),
-    ("RC", (2,), "V"),
-    ("B", (2,), "V"),
-    ("M1s", (6, 1,), "S"),
+    ("B", (0,), "V"),
     ("S1", (3, 1,), "S"),
-    ("M1v", (6,), "V"),
-    ("C", (2,), "V"),
-    ("Ls", (7,), "S"),
-    ("M2p", (4, 1,), "PE"),
+    ("M1p", (5, 0,), "PE"),
+    ("M1p", (5, 1,), "PE"),
     ("S1", (4, 0,), "S"),
+    ("NM", (2,), "V"),
     ("NM", (3,), "V"),
-    ("A", (3,), "V"),
-    ("S1", (4, 1,), "S"),
-    ("M2p", (5, 0,), "PE"),
-    ("S2", (3,), "S"),
-    ("M2p", (5, 1,), "PE"),
     ("Lv", (7,), "V"),
-    ("NM", (4,), "V"),
-    ("A", (4,), "V"),
+    ("M2p", (4, 1,), "PE"),
+    ("M1s", (5, 0,), "S"),
+    ("C", (0,), "V"),
+    ("S2", (2,), "S"),
     ("M1p", (7, 0,), "PE"),
-    ("SQ", (3,), "S"),
-    ("S2", (4,), "S"),
+    ("A", (2,), "V"),
     ("M1p", (7, 1,), "PE"),
-    ("RC", (3,), "V"),
-    ("B", (3,), "V"),
+    ("M1s", (5, 1,), "S"),
+    ("SQ", (2,), "S"),
+    ("A", (3,), "V"),
+    ("S2", (3,), "S"),
+    ("B", (2,), "V"),
+    ("S1", (4, 1,), "S"),
+    ("SQ", (3,), "S"),
+    ("M1v", (5,), "V"),
+    ("Ls", (6,), "S"),
+    ("C", (2,), "V"),
     ("M1s", (7, 0,), "S"),
-    ("C", (3,), "V"),
+    ("M2p", (5, 0,), "PE"),
     ("M1s", (7, 1,), "S"),
-    ("SQ", (4,), "S"),
+    ("B", (3,), "V"),
+    ("M2p", (5, 1,), "PE"),
     ("S1", (5, 0,), "S"),
-    ("M1v", (7,), "V"),
-    ("RC", (4,), "V"),
-    ("B", (4,), "V"),
     ("S1", (5, 1,), "S"),
-    ("M2p", (6, 0,), "PE"),
-    ("M2p", (6, 1,), "PE"),
-    ("S1", (6, 0,), "S"),
+    ("NM", (4,), "V"),
+    ("Lv", (6,), "V"),
+    ("C", (3,), "V"),
+    ("S2", (4,), "S"),
+    ("M1p", (6, 0,), "PE"),
+    ("A", (4,), "V"),
+    ("M1p", (6, 1,), "PE"),
+    ("M1s", (6, 0,), "S"),
+    ("SQ", (4,), "S"),
     ("NM", (5,), "V"),
+    ("M1v", (7,), "V"),
+    ("M1s", (6, 1,), "S"),
     ("A", (5,), "V"),
     ("S2", (5,), "S"),
     ("M2p", (7, 0,), "PE"),
-    ("C", (4,), "V"),
-    ("SQ", (5,), "S"),
-    ("S1", (6, 1,), "S"),
-    ("RC", (5,), "V"),
-    ("B", (5,), "V"),
-    ("S1", (7, 0,), "S"),
+    ("B", (4,), "V"),
     ("M2p", (7, 1,), "PE"),
+    ("S1", (7, 0,), "S"),
+    ("SQ", (5,), "S"),
+    ("M1v", (6,), "V"),
     ("S1", (7, 1,), "S"),
-    ("NM", (6,), "V"),
-    ("A", (6,), "V"),
-    ("S2", (6,), "S"),
-    ("C", (5,), "V"),
-    ("SQ", (6,), "S"),
+    ("C", (4,), "V"),
+    ("M2p", (6, 0,), "PE"),
+    ("B", (5,), "V"),
+    ("M2p", (6, 1,), "PE"),
+    ("S1", (6, 0,), "S"),
+    ("S1", (6, 1,), "S"),
     ("NM", (7,), "V"),
-    ("A", (7,), "V"),
+    ("C", (5,), "V"),
     ("S2", (7,), "S"),
-    ("RC", (6,), "V"),
-    ("B", (6,), "V"),
+    ("NM", (6,), "V"),
+    ("A", (7,), "V"),
+    ("S2", (6,), "S"),
+    ("A", (6,), "V"),
     ("SQ", (7,), "S"),
-    ("C", (6,), "V"),
-    ("RC", (7,), "V"),
+    ("SQ", (6,), "S"),
     ("B", (7,), "V"),
+    ("B", (6,), "V"),
     ("C", (7,), "V"),
+    ("C", (6,), "V"),
 )
 
 
@@ -217,46 +211,55 @@ def tile_gcn_pb_kernel(tc, lap, feat, w, gamma, beta, out):
         ypool = ctx.enter_context(tc.tile_pool(name="ypool", bufs=4))
         opool = ctx.enter_context(tc.tile_pool(name="opool", bufs=4))
         small = ctx.enter_context(tc.tile_pool(name="small", bufs=6))
-        psum = ctx.enter_context(tc.psum_pool(name="psum", bufs=2))
+        psum = ctx.enter_context(tc.psum_pool(name="psum", bufs=6))
         if MANUAL:
             ctx.enter_context(tc.manual_schedule())
 
+        gb_row = keep.tile([P, 2 * D], BF16)
+        nc.vector.memset(gb_row[:], 0.0)
+        nc.scalar.dma_start(out=gb_row[0:1, 0:D], in_=gamma.rearrange("(o d) -> o d", o=1))
+        nc.scalar.dma_start(out=gb_row[0:1, D : 2 * D], in_=beta.rearrange("(o d) -> o d", o=1))
         eps_t = keep.tile([P, 1], F32)
         nc.vector.memset(eps_t[:], EPS)
         warm = keep.tile([P, 1], F32)
-        nc.scalar.activation(out=warm[:], in_=eps_t[:], func=ACT.Sqrt)
+        nc.scalar.activation(out=warm[:], in_=eps_t[:], func=ACT.Abs_reciprocal_sqrt)
         ident = keep.tile([P, P], F32)
         make_identity(nc, ident[:])
         ones = keep.tile([P, P], BF16)
         nc.vector.memset(ones[:], 1.0)
-        gb_row = keep.tile([P, 2 * D], BF16)
-        nc.vector.memset(gb_row[:], 0.0)
-        nc.sync.dma_start(out=gb_row[0:1, 0:D], in_=gamma.rearrange("(o d) -> o d", o=1))
-        nc.sync.dma_start(out=gb_row[0:1, D : 2 * D], in_=beta.rearrange("(o d) -> o d", o=1))
 
         fr = keep.tile([P, 2, 4, D], BF16)
         lap_sb = keep.tile([P, NT, N], BF16)
         w_sb = keep.tile([P, NT, D], BF16)
         lap_v = lap.rearrange("(p t) j -> p t j", t=NT)
 
-        def load_w():
-            for k in range(4):
-                nc.sync.dma_start(
-                    out=w_sb[:, 2 * k : 2 * k + 2, :],
-                    in_=w[256 * k : 256 * k + 256, :].rearrange("(t p) d -> p t d", p=P),
-                )
+        def load_w(k):
+            nc.sync.dma_start(
+                out=w_sb[:, 2 * k : 2 * k + 2, :],
+                in_=w[256 * k : 256 * k + 256, :].rearrange("(t p) d -> p t d", p=P),
+            )
 
-        for g in range(2):
-            for u in range(2):
-                r0 = 512 * g + 256 * u
-                nc.sync.dma_start(
-                    out=fr[:, g, 2 * u : 2 * u + 2, :],
-                    in_=feat[r0 : r0 + 256, :].rearrange("(q e) c -> q e c", e=2),
-                )
-        nc.sync.dma_start(out=lap_sb[:, 0:2, :], in_=lap_v[:, 0:2, :])
-        load_w()
-        nc.sync.dma_start(out=lap_sb[:, 2:4, :], in_=lap_v[:, 2:4, :])
-        nc.sync.dma_start(out=lap_sb[:, 4:8, :], in_=lap_v[:, 4:8, :])
+        def load_f(g, u):
+            r0 = 512 * g + 256 * u
+            nc.sync.dma_start(
+                out=fr[:, g, 2 * u : 2 * u + 2, :],
+                in_=feat[r0 : r0 + 256, :].rearrange("(q e) c -> q e c", e=2),
+            )
+
+        def load_l(t0, t1):
+            nc.sync.dma_start(out=lap_sb[:, t0:t1, :], in_=lap_v[:, t0:t1, :])
+
+        load_f(0, 0)
+        load_f(0, 1)
+        load_l(0, 2)
+        load_f(1, 0)
+        load_f(1, 1)
+        load_w(0)
+        load_w(1)
+        load_w(2)
+        load_w(3)
+        load_l(2, 4)
+        load_l(4, 8)
         lap_w = lap_sb[:].bitcast(F32)
         w_w = w_sb[:].bitcast(F32)
 
@@ -274,7 +277,6 @@ def tile_gcn_pb_kernel(tc, lap, feat, w, gamma, beta, out):
         mg = keep.tile([P, NT, 2, P, 4], BF16, align_bytes=64)
         m_codes = keep.tile([P, NT, 2, P], U32, align_bytes=64)
         m_sc = keep.tile([P, NT, 2, P], U8, align_bytes=64)
-        junk = keep.tile([P, D], BF16)
         out_v = out.rearrange("(p t) o -> p t o", t=NT)
         live = {}
 
@@ -316,7 +318,7 @@ def tile_gcn_pb_kernel(tc, lap, feat, w, gamma, beta, out):
 
         def op_Lp(a, eng):
             it = a[0]
-            tp = psum.tile([P, 2, 2, P], F32, name="tp", tag="tp", bufs=2)
+            tp = psum.tile([P, 2, 2, P], F32, name="tp", tag="ps")
             for g in range(2):
                 for u in range(2):
                     c0 = 256 * g + 128 * u
@@ -337,7 +339,7 @@ def tile_gcn_pb_kernel(tc, lap, feat, w, gamma, beta, out):
 
         def op_Wp(a, eng):
             pr, g2 = a
-            tp = psum.tile([P, 2, 2, P], F32, name="tp", tag="tp", bufs=2)
+            tp = psum.tile([P, 2, 2, P], F32, name="tp", tag="ps")
             for b in range(2):
                 for u in range(2):
                     c0 = 256 * g2 + 128 * u
@@ -359,7 +361,7 @@ def tile_gcn_pb_kernel(tc, lap, feat, w, gamma, beta, out):
 
         def op_M1p(a, eng):
             it, g2 = a
-            mp = psum.tile([P, 4, P], F32, name="mp", tag="mp", bufs=2)
+            mp = psum.tile([P, 4, P], F32, name="mp", tag="ps")
             for t2 in range(4):
                 cs = slice((4 * g2 + t2) * P, (4 * g2 + t2 + 1) * P)
                 for g in range(2):
@@ -388,7 +390,7 @@ def tile_gcn_pb_kernel(tc, lap, feat, w, gamma, beta, out):
 
         def op_M2p(a, eng):
             it, h = a
-            yp = psum.tile([P, 512], F32, name="yp", tag="yp", bufs=2)
+            yp = psum.tile([P, 512], F32, name="yp", tag="ps")
             cs = slice(512 * h, 512 * h + 512)
             for g2 in range(2):
                 nc.tensor.matmul_mx(
@@ -424,6 +426,7 @@ def tile_gcn_pb_kernel(tc, lap, feat, w, gamma, beta, out):
         def op_S2(a, eng):
             it = a[0]
             ssq = small.tile([P, 1], F32, name="ssq", tag="ssq")
+            junk = keep.tile([P, D], BF16, name="junk", tag="junk")
             nc.scalar.activation(
                 out=junk[:], in_=live[("ysb", it)][:], func=ACT.Square, bias=live[("negmu", it)][:, 0:1], scale=1.0, accum_out=ssq[:]
             )
@@ -431,14 +434,10 @@ def tile_gcn_pb_kernel(tc, lap, feat, w, gamma, beta, out):
 
         def op_SQ(a, eng):
             it = a[0]
-            std = small.tile([P, 1], F32, name="std", tag="std")
-            nc.scalar.activation(out=std[:], in_=live[("ssq", it)][:], func=ACT.Sqrt, bias=eps_t[:, 0:1], scale=1.0 / D)
-            live[("std", it)] = std
-
-        def op_RC(a, eng):
-            it = a[0]
             rstd = small.tile([P, 1], F32, name="rstd", tag="rstd")
-            nc.vector.reciprocal(out=rstd[:], in_=live[("std", it)][:])
+            nc.scalar.activation(
+                out=rstd[:], in_=live[("ssq", it)][:], func=ACT.Abs_reciprocal_sqrt, bias=eps_t[:, 0:1], scale=1.0 / D
+            )
             live[("rstd", it)] = rstd
 
         def op_A(a, eng):
@@ -459,13 +458,17 @@ def tile_gcn_pb_kernel(tc, lap, feat, w, gamma, beta, out):
         def op_C(a, eng):
             it = a[0]
             z = live[("z", it)]
-            nc.vector.scalar_tensor_tensor(out=z[:], in0=z[:], scalar=SLOPE, in1=z[:], op0=ALU.mult, op1=ALU.max)
-            nc.sync.dma_start(out=out_v[:, it, :], in_=z[:])
+            pieces = LAST_PIECES if it == LAST_TILE else 1
+            width = D // pieces
+            for c in range(pieces):
+                cs = slice(c * width, (c + 1) * width)
+                nc.vector.scalar_tensor_tensor(out=z[:, cs], in0=z[:, cs], scalar=SLOPE, in1=z[:, cs], op0=ALU.mult, op1=ALU.max)
+                nc.sync.dma_start(out=out_v[:, it, cs], in_=z[:, cs])
 
         table = {
             "GBp": op_GBp, "RG": op_RG, "FQ": op_FQ, "Lp": op_Lp, "Ls": op_Ls, "Lv": op_Lv, "Wp": op_Wp, "Ws": op_Ws,
             "Wv": op_Wv, "M1p": op_M1p, "M1s": op_M1s, "M1v": op_M1v, "M2p": op_M2p, "S1": op_S1, "NM": op_NM,
-            "S2": op_S2, "SQ": op_SQ, "RC": op_RC, "A": op_A, "B": op_B, "C": op_C,
+            "S2": op_S2, "SQ": op_SQ, "A": op_A, "B": op_B, "C": op_C,
         }
         for kind, args, eng in ORDER:
             table[kind](args, eng)

@@ -30,6 +30,8 @@ ORDER = (
     ("RG", (0, 0, 1,), "S"),
     ("FQ", (0, 1,), "V"),
     ("Lp", (0,), "PE"),
+    ("GBp", (0,), "PE"),
+    ("GBp", (1,), "PE"),
     ("Ls", (1,), "S"),
     ("FQ", (0, 0,), "V"),
     ("Ls", (0,), "S"),
@@ -41,10 +43,8 @@ ORDER = (
     ("Wp", (0, 1,), "PE"),
     ("RG", (1, 1, 1,), "V"),
     ("Ws", (0, 0,), "S"),
-    ("GBp", (0,), "PE"),
     ("FQ", (1, 0,), "V"),
     ("Ws", (0, 1,), "S"),
-    ("GBp", (1,), "PE"),
     ("FQ", (1, 1,), "V"),
     ("Wp", (1, 0,), "PE"),
     ("Lv", (0,), "V"),

@@ -19,188 +19,188 @@ EPS = 1e-5
 SLOPE = 0.1
 FLOPS = 2 * 2 * N * N * D
 MANUAL = True
-LAST_TILE = 6
+LAST_TILE = 7
 LAST_PIECES = 2
 
 ORDER = (
-    ("RG", (0, 1, 0,), "V"),
-    ("RG", (0, 0, 0,), "S"),
-    ("RG", (0, 1, 1,), "V"),
-    ("Lp", (1,), "PE"),
-    ("RG", (0, 0, 1,), "S"),
-    ("FQ", (0, 1,), "V"),
     ("Lp", (0,), "PE"),
-    ("GBp", (0,), "PE"),
-    ("GBp", (1,), "PE"),
-    ("Ls", (1,), "S"),
-    ("FQ", (0, 0,), "V"),
-    ("Ls", (0,), "S"),
-    ("Lv", (1,), "V"),
-    ("RG", (1, 0, 1,), "S"),
-    ("RG", (1, 0, 0,), "V"),
-    ("RG", (1, 1, 0,), "V"),
     ("Wp", (0, 0,), "PE"),
     ("Wp", (0, 1,), "PE"),
-    ("RG", (1, 1, 1,), "V"),
-    ("Ws", (0, 0,), "S"),
-    ("FQ", (1, 0,), "V"),
-    ("Ws", (0, 1,), "S"),
-    ("FQ", (1, 1,), "V"),
+    ("GBp", (0,), "PE"),
+    ("GBp", (1,), "PE"),
     ("Wp", (1, 0,), "PE"),
-    ("Lv", (0,), "V"),
     ("Wp", (1, 1,), "PE"),
-    ("Ws", (1, 0,), "S"),
     ("Wp", (2, 0,), "PE"),
-    ("Ws", (1, 1,), "S"),
-    ("M1p", (1, 0,), "PE"),
-    ("Wv", (0, 0,), "V"),
-    ("Ws", (2, 0,), "S"),
-    ("M1p", (1, 1,), "PE"),
-    ("Wv", (0, 1,), "V"),
-    ("M1s", (1, 0,), "S"),
     ("Wp", (2, 1,), "PE"),
-    ("M1s", (1, 1,), "V"),
     ("Wp", (3, 0,), "PE"),
-    ("Ws", (2, 1,), "S"),
     ("Wp", (3, 1,), "PE"),
-    ("M1v", (1,), "V"),
+    ("Lp", (1,), "PE"),
+    ("RG", (0, 0, 0,), "S"),
+    ("RG", (0, 0, 1,), "S"),
+    ("RG", (0, 1, 0,), "S"),
+    ("RG", (1, 0, 1,), "S"),
+    ("Ls", (0,), "S"),
+    ("Ws", (0, 0,), "S"),
+    ("Ws", (0, 1,), "S"),
+    ("Ws", (1, 0,), "S"),
+    ("Ws", (1, 1,), "S"),
+    ("Ws", (2, 0,), "S"),
     ("Ws", (3, 0,), "S"),
-    ("Lp", (3,), "PE"),
-    ("Ws", (3, 1,), "V"),
-    ("Lp", (2,), "PE"),
+    ("Ws", (3, 1,), "S"),
+    ("Ls", (1,), "S"),
+    ("RG", (0, 1, 1,), "V"),
+    ("FQ", (0, 0,), "V"),
+    ("FQ", (0, 1,), "V"),
+    ("RG", (1, 0, 0,), "V"),
+    ("RG", (1, 1, 0,), "V"),
+    ("RG", (1, 1, 1,), "V"),
+    ("FQ", (1, 0,), "V"),
+    ("FQ", (1, 1,), "V"),
+    ("Lv", (0,), "V"),
+    ("Wv", (0, 0,), "V"),
+    ("Wv", (0, 1,), "V"),
+    ("Ws", (2, 1,), "V"),
     ("Wv", (1, 0,), "V"),
-    ("M1p", (0, 0,), "PE"),
     ("Wv", (1, 1,), "V"),
-    ("Ls", (2,), "S"),
+    ("Lv", (1,), "V"),
+    ("M1p", (0, 0,), "PE"),
     ("M1p", (0, 1,), "PE"),
-    ("Ls", (3,), "V"),
+    ("Lp", (2,), "PE"),
+    ("M1p", (1, 0,), "PE"),
+    ("M1p", (1, 1,), "PE"),
     ("M1s", (0, 0,), "S"),
-    ("M2p", (1, 0,), "PE"),
     ("M1s", (0, 1,), "S"),
-    ("Lv", (2,), "V"),
-    ("M2p", (1, 1,), "PE"),
-    ("Lv", (3,), "V"),
-    ("S1", (1, 0,), "S"),
-    ("Lp", (4,), "PE"),
+    ("Ls", (2,), "S"),
+    ("M1s", (1, 0,), "S"),
     ("M1v", (0,), "V"),
-    ("S1", (1, 1,), "S"),
-    ("M1p", (3, 0,), "PE"),
-    ("Ls", (4,), "S"),
-    ("M1p", (3, 1,), "PE"),
-    ("NM", (1,), "V"),
-    ("M1s", (3, 0,), "V"),
-    ("M1p", (2, 0,), "PE"),
-    ("S2", (1,), "S"),
-    ("Lv", (4,), "V"),
-    ("M1p", (2, 1,), "PE"),
-    ("A", (1,), "V"),
+    ("M1s", (1, 1,), "V"),
+    ("Lv", (2,), "V"),
+    ("M1v", (1,), "V"),
     ("M2p", (0, 0,), "PE"),
-    ("M1s", (3, 1,), "S"),
     ("M2p", (0, 1,), "PE"),
-    ("M1s", (2, 0,), "V"),
-    ("SQ", (1,), "S"),
-    ("M1p", (4, 0,), "PE"),
+    ("Lp", (3,), "PE"),
+    ("M1p", (2, 0,), "PE"),
+    ("M1p", (2, 1,), "PE"),
+    ("M2p", (1, 0,), "PE"),
+    ("M2p", (1, 1,), "PE"),
+    ("Lp", (4,), "PE"),
     ("S1", (0, 0,), "S"),
-    ("M1v", (3,), "V"),
-    ("M1s", (2, 1,), "V"),
-    ("M1p", (4, 1,), "PE"),
     ("S1", (0, 1,), "S"),
-    ("Lp", (5,), "PE"),
-    ("B", (1,), "V"),
-    ("M1s", (4, 0,), "S"),
-    ("M2p", (3, 0,), "PE"),
-    ("M1s", (4, 1,), "S"),
-    ("M1v", (2,), "V"),
-    ("M2p", (3, 1,), "PE"),
-    ("Ls", (5,), "S"),
+    ("Ls", (3,), "S"),
     ("NM", (0,), "V"),
-    ("C", (1,), "V"),
-    ("Lp", (6,), "PE"),
-    ("S1", (3, 0,), "S"),
-    ("M2p", (2, 0,), "PE"),
-    ("S2", (0,), "S"),
+    ("M1s", (2, 0,), "V"),
+    ("M1s", (2, 1,), "V"),
+    ("Lv", (3,), "V"),
     ("A", (0,), "V"),
+    ("M1v", (2,), "V"),
+    ("M1p", (3, 0,), "PE"),
+    ("M1p", (3, 1,), "PE"),
+    ("M2p", (2, 0,), "PE"),
     ("M2p", (2, 1,), "PE"),
-    ("Lp", (7,), "PE"),
-    ("S1", (2, 0,), "S"),
-    ("M1v", (4,), "V"),
-    ("Lv", (5,), "V"),
+    ("Lp", (5,), "PE"),
+    ("S2", (0,), "S"),
+    ("S1", (1, 0,), "S"),
+    ("S1", (1, 1,), "S"),
     ("SQ", (0,), "S"),
-    ("Ls", (7,), "V"),
-    ("S1", (2, 1,), "S"),
-    ("M2p", (4, 0,), "PE"),
+    ("Ls", (4,), "S"),
+    ("M1s", (3, 0,), "S"),
+    ("M1s", (3, 1,), "S"),
+    ("NM", (1,), "V"),
     ("B", (0,), "V"),
-    ("S1", (3, 1,), "S"),
+    ("Lv", (4,), "V"),
+    ("A", (1,), "V"),
+    ("M1v", (3,), "V"),
+    ("C", (0,), "V"),
+    ("M1p", (4, 0,), "PE"),
+    ("M1p", (4, 1,), "PE"),
+    ("M2p", (3, 0,), "PE"),
+    ("M2p", (3, 1,), "PE"),
+    ("Lp", (6,), "PE"),
+    ("S2", (1,), "S"),
+    ("S1", (2, 0,), "S"),
+    ("S1", (2, 1,), "S"),
+    ("SQ", (1,), "S"),
+    ("Ls", (5,), "S"),
+    ("M1s", (4, 0,), "S"),
+    ("NM", (2,), "V"),
+    ("M1s", (4, 1,), "V"),
+    ("B", (1,), "V"),
+    ("Lv", (5,), "V"),
+    ("A", (2,), "V"),
+    ("M1v", (4,), "V"),
+    ("C", (1,), "V"),
     ("M1p", (5, 0,), "PE"),
     ("M1p", (5, 1,), "PE"),
-    ("S1", (4, 0,), "S"),
-    ("NM", (2,), "V"),
-    ("NM", (3,), "V"),
-    ("Lv", (7,), "V"),
+    ("M2p", (4, 0,), "PE"),
     ("M2p", (4, 1,), "PE"),
-    ("M1s", (5, 0,), "S"),
-    ("C", (0,), "V"),
+    ("Lp", (7,), "PE"),
     ("S2", (2,), "S"),
-    ("M1p", (7, 0,), "PE"),
-    ("A", (2,), "V"),
-    ("M1p", (7, 1,), "PE"),
-    ("M1s", (5, 1,), "S"),
+    ("S1", (3, 0,), "S"),
+    ("S1", (3, 1,), "S"),
     ("SQ", (2,), "S"),
-    ("A", (3,), "V"),
-    ("S2", (3,), "S"),
+    ("Ls", (6,), "S"),
+    ("M1s", (5, 0,), "S"),
+    ("M1s", (5, 1,), "S"),
+    ("NM", (3,), "V"),
     ("B", (2,), "V"),
+    ("Lv", (6,), "V"),
+    ("A", (3,), "V"),
+    ("M1v", (5,), "V"),
+    ("C", (2,), "V"),
+    ("M1p", (6, 0,), "PE"),
+    ("M1p", (6, 1,), "PE"),
+    ("M2p", (5, 0,), "PE"),
+    ("M2p", (5, 1,), "PE"),
+    ("S2", (3,), "S"),
+    ("S1", (4, 0,), "S"),
     ("S1", (4, 1,), "S"),
     ("SQ", (3,), "S"),
-    ("M1v", (5,), "V"),
-    ("Ls", (6,), "S"),
-    ("C", (2,), "V"),
-    ("M1s", (7, 0,), "S"),
-    ("M2p", (5, 0,), "PE"),
-    ("M1s", (7, 1,), "S"),
+    ("Ls", (7,), "S"),
+    ("M1s", (6, 0,), "S"),
+    ("M1s", (6, 1,), "S"),
+    ("NM", (4,), "V"),
     ("B", (3,), "V"),
-    ("M2p", (5, 1,), "PE"),
+    ("Lv", (7,), "V"),
+    ("A", (4,), "V"),
+    ("M1v", (6,), "V"),
+    ("C", (3,), "V"),
+    ("M1p", (7, 0,), "PE"),
+    ("M1p", (7, 1,), "PE"),
+    ("M2p", (6, 0,), "PE"),
+    ("M2p", (6, 1,), "PE"),
+    ("S2", (4,), "S"),
     ("S1", (5, 0,), "S"),
     ("S1", (5, 1,), "S"),
-    ("NM", (4,), "V"),
-    ("Lv", (6,), "V"),
-    ("C", (3,), "V"),
-    ("S2", (4,), "S"),
-    ("M1p", (6, 0,), "PE"),
-    ("A", (4,), "V"),
-    ("M1p", (6, 1,), "PE"),
-    ("M1s", (6, 0,), "S"),
     ("SQ", (4,), "S"),
+    ("M1s", (7, 0,), "S"),
+    ("M1s", (7, 1,), "S"),
     ("NM", (5,), "V"),
-    ("M1v", (7,), "V"),
-    ("M1s", (6, 1,), "S"),
-    ("A", (5,), "V"),
-    ("S2", (5,), "S"),
-    ("M2p", (7, 0,), "PE"),
     ("B", (4,), "V"),
-    ("M2p", (7, 1,), "PE"),
-    ("S1", (7, 0,), "S"),
-    ("SQ", (5,), "S"),
-    ("M1v", (6,), "V"),
-    ("S1", (7, 1,), "S"),
+    ("A", (5,), "V"),
+    ("M1v", (7,), "V"),
     ("C", (4,), "V"),
-    ("M2p", (6, 0,), "PE"),
-    ("B", (5,), "V"),
-    ("M2p", (6, 1,), "PE"),
+    ("M2p", (7, 0,), "PE"),
+    ("M2p", (7, 1,), "PE"),
+    ("S2", (5,), "S"),
     ("S1", (6, 0,), "S"),
     ("S1", (6, 1,), "S"),
-    ("NM", (7,), "V"),
-    ("C", (5,), "V"),
-    ("S2", (7,), "S"),
+    ("SQ", (5,), "S"),
     ("NM", (6,), "V"),
-    ("A", (7,), "V"),
-    ("S2", (6,), "S"),
+    ("B", (5,), "V"),
     ("A", (6,), "V"),
-    ("SQ", (7,), "S"),
+    ("C", (5,), "V"),
+    ("S2", (6,), "S"),
+    ("S1", (7, 0,), "S"),
+    ("S1", (7, 1,), "S"),
     ("SQ", (6,), "S"),
-    ("B", (7,), "V"),
+    ("NM", (7,), "V"),
     ("B", (6,), "V"),
-    ("C", (7,), "V"),
+    ("A", (7,), "V"),
     ("C", (6,), "V"),
+    ("S2", (7,), "S"),
+    ("SQ", (7,), "S"),
+    ("B", (7,), "V"),
+    ("C", (7,), "V"),
 )
 
 

@@ -14,461 +14,323 @@ ACT = mybir.ActivationFunctionType
 P = 128
 N = 1024
 D = 1024
-NT = N // P
+TILES = N // P
+PACK = 4
+PASSES = 2
+BANK = 512
 EPS = 1e-5
 SLOPE = 0.1
 FLOPS = 2 * 2 * N * N * D
-MANUAL = True
-LAST_TILE = 7
-LAST_PIECES = 2
 
-ORDER = (
-    ("Lp", (0,), "PE"),
-    ("Wp", (0, 0,), "PE"),
-    ("Wp", (0, 1,), "PE"),
-    ("GBp", (0,), "PE"),
-    ("GBp", (1,), "PE"),
-    ("Wp", (1, 0,), "PE"),
-    ("Wp", (1, 1,), "PE"),
-    ("Wp", (2, 0,), "PE"),
-    ("Wp", (2, 1,), "PE"),
-    ("Wp", (3, 0,), "PE"),
-    ("Wp", (3, 1,), "PE"),
-    ("Lp", (1,), "PE"),
-    ("RG", (0, 0, 0,), "S"),
-    ("RG", (0, 0, 1,), "S"),
-    ("RG", (0, 1, 0,), "S"),
-    ("RG", (1, 0, 1,), "S"),
-    ("Ls", (0,), "S"),
-    ("Ws", (0, 0,), "S"),
-    ("Ws", (0, 1,), "S"),
-    ("Ws", (1, 0,), "S"),
-    ("Ws", (1, 1,), "S"),
-    ("Ws", (2, 0,), "S"),
-    ("Ws", (3, 0,), "S"),
-    ("Ws", (3, 1,), "S"),
-    ("Ls", (1,), "S"),
-    ("RG", (0, 1, 1,), "V"),
-    ("FQ", (0, 0,), "V"),
-    ("FQ", (0, 1,), "V"),
-    ("RG", (1, 0, 0,), "V"),
-    ("RG", (1, 1, 0,), "V"),
-    ("RG", (1, 1, 1,), "V"),
-    ("FQ", (1, 0,), "V"),
-    ("FQ", (1, 1,), "V"),
-    ("Lv", (0,), "V"),
-    ("Wv", (0, 0,), "V"),
-    ("Wv", (0, 1,), "V"),
-    ("Ws", (2, 1,), "V"),
-    ("Wv", (1, 0,), "V"),
-    ("Wv", (1, 1,), "V"),
-    ("Lv", (1,), "V"),
-    ("M1p", (0, 0,), "PE"),
-    ("M1p", (0, 1,), "PE"),
-    ("Lp", (2,), "PE"),
-    ("M1p", (1, 0,), "PE"),
-    ("M1p", (1, 1,), "PE"),
-    ("M1s", (0, 0,), "S"),
-    ("M1s", (0, 1,), "S"),
-    ("Ls", (2,), "S"),
-    ("M1s", (1, 0,), "S"),
-    ("M1v", (0,), "V"),
-    ("M1s", (1, 1,), "V"),
-    ("Lv", (2,), "V"),
-    ("M1v", (1,), "V"),
-    ("M2p", (0, 0,), "PE"),
-    ("M2p", (0, 1,), "PE"),
-    ("Lp", (3,), "PE"),
-    ("M1p", (2, 0,), "PE"),
-    ("M1p", (2, 1,), "PE"),
-    ("M2p", (1, 0,), "PE"),
-    ("M2p", (1, 1,), "PE"),
-    ("Lp", (4,), "PE"),
-    ("S1", (0, 0,), "S"),
-    ("S1", (0, 1,), "S"),
-    ("Ls", (3,), "S"),
-    ("NM", (0,), "V"),
-    ("M1s", (2, 0,), "V"),
-    ("M1s", (2, 1,), "V"),
-    ("Lv", (3,), "V"),
-    ("A", (0,), "V"),
-    ("M1v", (2,), "V"),
-    ("M1p", (3, 0,), "PE"),
-    ("M1p", (3, 1,), "PE"),
-    ("M2p", (2, 0,), "PE"),
-    ("M2p", (2, 1,), "PE"),
-    ("Lp", (5,), "PE"),
-    ("S2", (0,), "S"),
-    ("S1", (1, 0,), "S"),
-    ("S1", (1, 1,), "S"),
-    ("SQ", (0,), "S"),
-    ("Ls", (4,), "S"),
-    ("M1s", (3, 0,), "S"),
-    ("M1s", (3, 1,), "S"),
-    ("NM", (1,), "V"),
-    ("B", (0,), "V"),
-    ("Lv", (4,), "V"),
-    ("A", (1,), "V"),
-    ("M1v", (3,), "V"),
-    ("C", (0,), "V"),
-    ("M1p", (4, 0,), "PE"),
-    ("M1p", (4, 1,), "PE"),
-    ("M2p", (3, 0,), "PE"),
-    ("M2p", (3, 1,), "PE"),
-    ("Lp", (6,), "PE"),
-    ("S2", (1,), "S"),
-    ("S1", (2, 0,), "S"),
-    ("S1", (2, 1,), "S"),
-    ("SQ", (1,), "S"),
-    ("Ls", (5,), "S"),
-    ("M1s", (4, 0,), "S"),
-    ("NM", (2,), "V"),
-    ("M1s", (4, 1,), "V"),
-    ("B", (1,), "V"),
-    ("Lv", (5,), "V"),
-    ("A", (2,), "V"),
-    ("M1v", (4,), "V"),
-    ("C", (1,), "V"),
-    ("M1p", (5, 0,), "PE"),
-    ("M1p", (5, 1,), "PE"),
-    ("M2p", (4, 0,), "PE"),
-    ("M2p", (4, 1,), "PE"),
-    ("Lp", (7,), "PE"),
-    ("S2", (2,), "S"),
-    ("S1", (3, 0,), "S"),
-    ("S1", (3, 1,), "S"),
-    ("SQ", (2,), "S"),
-    ("Ls", (6,), "S"),
-    ("M1s", (5, 0,), "S"),
-    ("M1s", (5, 1,), "S"),
-    ("NM", (3,), "V"),
-    ("B", (2,), "V"),
-    ("Lv", (6,), "V"),
-    ("A", (3,), "V"),
-    ("M1v", (5,), "V"),
-    ("C", (2,), "V"),
-    ("M1p", (6, 0,), "PE"),
-    ("M1p", (6, 1,), "PE"),
-    ("M2p", (5, 0,), "PE"),
-    ("M2p", (5, 1,), "PE"),
-    ("S2", (3,), "S"),
-    ("S1", (4, 0,), "S"),
-    ("S1", (4, 1,), "S"),
-    ("SQ", (3,), "S"),
-    ("Ls", (7,), "S"),
-    ("M1s", (6, 0,), "S"),
-    ("M1s", (6, 1,), "S"),
-    ("NM", (4,), "V"),
-    ("B", (3,), "V"),
-    ("Lv", (7,), "V"),
-    ("A", (4,), "V"),
-    ("M1v", (6,), "V"),
-    ("C", (3,), "V"),
-    ("M1p", (7, 0,), "PE"),
-    ("M1p", (7, 1,), "PE"),
-    ("M2p", (6, 0,), "PE"),
-    ("M2p", (6, 1,), "PE"),
-    ("S2", (4,), "S"),
-    ("S1", (5, 0,), "S"),
-    ("S1", (5, 1,), "S"),
-    ("SQ", (4,), "S"),
-    ("M1s", (7, 0,), "S"),
-    ("M1s", (7, 1,), "S"),
-    ("NM", (5,), "V"),
-    ("B", (4,), "V"),
-    ("A", (5,), "V"),
-    ("M1v", (7,), "V"),
-    ("C", (4,), "V"),
-    ("M2p", (7, 0,), "PE"),
-    ("M2p", (7, 1,), "PE"),
-    ("S2", (5,), "S"),
-    ("S1", (6, 0,), "S"),
-    ("S1", (6, 1,), "S"),
-    ("SQ", (5,), "S"),
-    ("NM", (6,), "V"),
-    ("B", (5,), "V"),
-    ("A", (6,), "V"),
-    ("C", (5,), "V"),
-    ("S2", (6,), "S"),
-    ("S1", (7, 0,), "S"),
-    ("S1", (7, 1,), "S"),
-    ("SQ", (6,), "S"),
-    ("NM", (7,), "V"),
-    ("B", (6,), "V"),
-    ("A", (7,), "V"),
-    ("C", (6,), "V"),
-    ("S2", (7,), "S"),
-    ("SQ", (7,), "S"),
-    ("B", (7,), "V"),
-    ("C", (7,), "V"),
-)
+DEPTH = 4
+W_ROUND = 1
+M_TILES_EMPTIED_BY_VECTOR = (2, 3)
+LAST_STORES = 2
 
 
 def tile_gcn_pb_kernel(tc, lap, feat, w, gamma, beta, out):
     nc = tc.nc
     with ExitStack() as ctx:
         keep = ctx.enter_context(tc.tile_pool(name="keep", bufs=1))
-        ypool = ctx.enter_context(tc.tile_pool(name="ypool", bufs=4))
-        opool = ctx.enter_context(tc.tile_pool(name="opool", bufs=4))
-        small = ctx.enter_context(tc.tile_pool(name="small", bufs=6))
+        rows = ctx.enter_context(tc.tile_pool(name="rows", bufs=4))
+        stats = ctx.enter_context(tc.tile_pool(name="stats", bufs=6))
         psum = ctx.enter_context(tc.psum_pool(name="psum", bufs=6))
-        if MANUAL:
-            ctx.enter_context(tc.manual_schedule())
+        ctx.enter_context(tc.manual_schedule())
 
         gb_row = keep.tile([P, 2 * D], BF16)
         nc.vector.memset(gb_row[:], 0.0)
         nc.scalar.dma_start(out=gb_row[0:1, 0:D], in_=gamma.rearrange("(o d) -> o d", o=1))
         nc.scalar.dma_start(out=gb_row[0:1, D : 2 * D], in_=beta.rearrange("(o d) -> o d", o=1))
-        eps_t = keep.tile([P, 1], F32)
-        nc.vector.memset(eps_t[:], EPS)
+        eps_col = keep.tile([P, 1], F32)
+        nc.vector.memset(eps_col[:], EPS)
         warm = keep.tile([P, 1], F32)
-        nc.scalar.activation(out=warm[:], in_=eps_t[:], func=ACT.Abs_reciprocal_sqrt)
+        nc.scalar.activation(out=warm[:], in_=eps_col[:], func=ACT.Abs_reciprocal_sqrt)
         ident = keep.tile([P, P], F32)
         make_identity(nc, ident[:])
         ones = keep.tile([P, P], BF16)
         nc.vector.memset(ones[:], 1.0)
 
-        fr = keep.tile([P, 2, 4, D], BF16)
-        lap_sb = keep.tile([P, NT, N], BF16)
-        w_sb = keep.tile([P, NT, D], BF16)
-        lap_v = lap.rearrange("(p t) j -> p t j", t=NT)
+        feat_raw = keep.tile([P, PASSES, PACK, D], BF16)
+        lap_sb = keep.tile([P, TILES, N], BF16)
+        w_sb = keep.tile([P, TILES, D], BF16)
+        lap_rows = lap.rearrange("(p t) j -> p t j", t=TILES)
 
-        def load_w(k):
-            nc.sync.dma_start(
-                out=w_sb[:, 2 * k : 2 * k + 2, :],
-                in_=w[256 * k : 256 * k + 256, :].rearrange("(t p) d -> p t d", p=P),
-            )
-
-        def load_f(g, u):
-            r0 = 512 * g + 256 * u
-            nc.sync.dma_start(
-                out=fr[:, g, 2 * u : 2 * u + 2, :],
-                in_=feat[r0 : r0 + 256, :].rearrange("(q e) c -> q e c", e=2),
-            )
-
-        def load_l(t0, t1):
-            nc.sync.dma_start(out=lap_sb[:, t0:t1, :], in_=lap_v[:, t0:t1, :])
-
-        load_f(0, 0)
-        load_f(0, 1)
-        load_l(0, 2)
-        load_f(1, 0)
-        load_f(1, 1)
-        load_w(0)
-        load_w(1)
-        load_w(2)
-        load_w(3)
-        load_l(2, 4)
-        load_l(4, 8)
-        lap_w = lap_sb[:].bitcast(F32)
-        w_w = w_sb[:].bitcast(F32)
-
-        fg = keep.tile([P, 2, D, 4], BF16, align_bytes=64)
-        f_codes = keep.tile([P, 2, D], U32, align_bytes=64)
-        f_sc = keep.tile([P, 2, D], U8, align_bytes=64)
-        lg = keep.tile([P, NT, 2, P, 4], BF16, align_bytes=64)
-        lg_w = lg[:].bitcast(F32)
-        l_codes = keep.tile([P, NT, 2, P], U32, align_bytes=64)
-        l_sc = keep.tile([P, NT, 2, P], U8, align_bytes=64)
-        wg = keep.tile([P, 2, D, 4], BF16, align_bytes=64)
-        wg_w = wg[:].bitcast(F32)
-        w_codes = keep.tile([P, 2, D], U32, align_bytes=64)
-        w_sc = keep.tile([P, 2, D], U8, align_bytes=64)
-        mg = keep.tile([P, NT, 2, P, 4], BF16, align_bytes=64)
-        m_codes = keep.tile([P, NT, 2, P], U32, align_bytes=64)
-        m_sc = keep.tile([P, NT, 2, P], U8, align_bytes=64)
-        out_v = out.rearrange("(p t) o -> p t o", t=NT)
-        live = {}
-
-        def copy_on(eng, dst, src):
-            if eng == "V":
-                nc.vector.tensor_copy(out=dst, in_=src)
-            else:
-                nc.scalar.copy(out=dst, in_=src)
-
-        def op_GBp(a, eng):
-            k = a[0]
-            bank = psum.tile([P, D], BF16, name="gb%d" % k, tag="gb%d" % k, bufs=1)
-            for h in range(2):
-                c0 = D * k + 512 * h
-                nc.tensor.matmul(
-                    out=bank[:, 512 * h : 512 * h + 512], lhsT=ones[:], rhs=gb_row[:, c0 : c0 + 512], start=True, stop=True
+        def load_feat(g):
+            for u in range(2):
+                first = 512 * g + 256 * u
+                nc.sync.dma_start(
+                    out=feat_raw[:, g, 2 * u : 2 * u + 2, :],
+                    in_=feat[first : first + 256, :].rearrange("(p e) d -> p e d", e=2),
                 )
-            live[("gb", k)] = bank
 
-        def op_RG(a, eng):
-            g, g2, u = a
-            c0 = 512 * g2 + 256 * u
-            src = fr[:, g, :, c0 : c0 + 256].rearrange("p t (c i e) -> p e c t i", i=4, e=2)
-            dst = fg[:, g, c0 : c0 + 256, :].rearrange("p (e c i) t -> p e c t i", e=2, i=4)
-            if eng == "V":
+        def load_lap(t0, t1):
+            nc.sync.dma_start(out=lap_sb[:, t0:t1, :], in_=lap_rows[:, t0:t1, :])
+
+        load_feat(0)
+        load_lap(0, 2)
+        load_feat(1)
+        for pair in range(TILES // 2):
+            nc.sync.dma_start(
+                out=w_sb[:, 2 * pair : 2 * pair + 2, :],
+                in_=w[256 * pair : 256 * pair + 256, :].rearrange("(t p) d -> p t d", p=P),
+            )
+        load_lap(2, 4)
+        load_lap(4, 8)
+        lap_words = lap_sb[:].bitcast(F32)
+        w_words = w_sb[:].bitcast(F32)
+
+        feat_grouped = keep.tile([P, PASSES, D, PACK], BF16, align_bytes=64)
+        feat_codes = keep.tile([P, PASSES, D], U32, align_bytes=64)
+        feat_scales = keep.tile([P, PASSES, D], U8, align_bytes=64)
+        lap_grouped = keep.tile([P, TILES, PASSES, P, PACK], BF16, align_bytes=64)
+        lap_grouped_words = lap_grouped[:].bitcast(F32)
+        lap_codes = keep.tile([P, TILES, PASSES, P], U32, align_bytes=64)
+        lap_scales = keep.tile([P, TILES, PASSES, P], U8, align_bytes=64)
+        w_grouped = keep.tile([P, PASSES, D, PACK], BF16, align_bytes=64)
+        w_grouped_words = w_grouped[:].bitcast(F32)
+        w_codes = keep.tile([P, PASSES, D], U32, align_bytes=64)
+        w_scales = keep.tile([P, PASSES, D], U8, align_bytes=64)
+        m_grouped = keep.tile([P, TILES, PASSES, P, PACK], BF16, align_bytes=64)
+        m_codes = keep.tile([P, TILES, PASSES, P], U32, align_bytes=64)
+        m_scales = keep.tile([P, TILES, PASSES, P], U8, align_bytes=64)
+        squares = keep.tile([P, D], BF16)
+        out_rows = out.rearrange("(p t) o -> p t o", t=TILES)
+        banks = {}
+        held = {}
+
+        def new_bank(shape):
+            return psum.tile(shape, F32, name="bank", tag="bank")
+
+        def regroup_feat(g, block, on_vector):
+            cols = slice(256 * block, 256 * block + 256)
+            src = feat_raw[:, g, :, cols].rearrange("p t (c i e) -> p e c t i", i=4, e=2)
+            dst = feat_grouped[:, g, cols, :].rearrange("p (e c i) t -> p e c t i", e=2, i=4)
+            if on_vector:
                 nc.vector.tensor_copy(out=dst, in_=src)
             else:
                 for e in range(2):
                     nc.scalar.copy(out=dst[:, e], in_=src[:, e])
 
-        def op_FQ(a, eng):
-            g, g2 = a
-            cs = slice(512 * g2, 512 * g2 + 512)
+        def quantise_feat(g, half):
+            cols = slice(BANK * half, BANK * half + BANK)
             nc.vector.quantize_mx(
-                out=f_codes[:, g, cs].bitcast(FP8X4),
-                scales=f_sc[:, g, cs],
-                in_=fg[:, g, cs, :].rearrange("p c t -> p (c t)"),
+                out=feat_codes[:, g, cols].bitcast(FP8X4),
+                scales=feat_scales[:, g, cols],
+                in_=feat_grouped[:, g, cols, :].rearrange("p c t -> p (c t)"),
             )
 
-        def op_Lp(a, eng):
-            it = a[0]
-            tp = psum.tile([P, 2, 2, P], F32, name="tp", tag="ps")
-            for g in range(2):
+        def transpose_lap(t):
+            bank = new_bank([P, PASSES, 2, P])
+            for g in range(PASSES):
                 for u in range(2):
-                    c0 = 256 * g + 128 * u
-                    nc.tensor.transpose(tp[:, g, u, :], lap_w[:, it, c0 : c0 + 128], ident[:])
-            live[("L", it)] = tp
+                    first = 256 * g + 128 * u
+                    nc.tensor.transpose(bank[:, g, u, :], lap_words[:, t, first : first + P], ident[:])
+            banks[("lap", t)] = bank
 
-        def op_Ls(a, eng):
-            it = a[0]
-            copy_on(eng, lg_w[:, it], live[("L", it)][:].rearrange("p g u i -> p g i u"))
+        def copy_lap(t):
+            nc.scalar.copy(out=lap_grouped_words[:, t], in_=banks[("lap", t)][:].rearrange("p g u i -> p g i u"))
 
-        def op_Lv(a, eng):
-            it = a[0]
+        def quantise_lap(t):
             nc.vector.quantize_mx(
-                out=l_codes[:, it].rearrange("p g i -> p (g i)").bitcast(FP8X4),
-                scales=l_sc[:, it].rearrange("p g i -> p (g i)"),
-                in_=lg[:, it].rearrange("p g i t -> p (g i t)"),
+                out=lap_codes[:, t].rearrange("p g i -> p (g i)").bitcast(FP8X4),
+                scales=lap_scales[:, t].rearrange("p g i -> p (g i)"),
+                in_=lap_grouped[:, t].rearrange("p g i t -> p (g i t)"),
             )
 
-        def op_Wp(a, eng):
-            pr, g2 = a
-            tp = psum.tile([P, 2, 2, P], F32, name="tp", tag="ps")
+        def transpose_w(pair, g):
+            bank = new_bank([P, 2, 2, P])
             for b in range(2):
                 for u in range(2):
-                    c0 = 256 * g2 + 128 * u
-                    nc.tensor.transpose(tp[:, u, b, :], w_w[:, 2 * pr + b, c0 : c0 + 128], ident[:])
-            live[("W", pr, g2)] = tp
+                    first = 256 * g + 128 * u
+                    nc.tensor.transpose(bank[:, u, b, :], w_words[:, 2 * pair + b, first : first + P], ident[:])
+            banks[("w", pair, g)] = bank
 
-        def op_Ws(a, eng):
-            pr, g2 = a
-            copy_on(eng, wg_w[:, g2, 256 * pr : 256 * pr + 256, :], live[("W", pr, g2)][:].rearrange("p u b o -> p (b o) u"))
-
-        def op_Wv(a, eng):
-            h, g2 = a
-            cs = slice(512 * h, 512 * h + 512)
-            nc.vector.quantize_mx(
-                out=w_codes[:, g2, cs].bitcast(FP8X4),
-                scales=w_sc[:, g2, cs],
-                in_=wg[:, g2, cs, :].rearrange("p c t -> p (c t)"),
+        def copy_w(pair, g):
+            nc.scalar.copy(
+                out=w_grouped_words[:, g, 256 * pair : 256 * pair + 256, :],
+                in_=banks[("w", pair, g)][:].rearrange("p u b o -> p (b o) u"),
             )
 
-        def op_M1p(a, eng):
-            it, g2 = a
-            mp = psum.tile([P, 4, P], F32, name="mp", tag="ps")
-            for t2 in range(4):
-                cs = slice((4 * g2 + t2) * P, (4 * g2 + t2 + 1) * P)
-                for g in range(2):
-                    nc.tensor.matmul_mx(
-                        out=mp[:, t2, :],
-                        lhsT=f_codes[:, g, cs].bitcast(FP8X4),
-                        lhsT_scale=f_sc[:, g, cs],
-                        rhs=l_codes[:, it, g, :].bitcast(FP8X4),
-                        rhs_scale=l_sc[:, it, g, :],
-                        start=(g == 0),
-                        stop=(g == 1),
-                    )
-            live[("M", it, g2)] = mp
-
-        def op_M1s(a, eng):
-            it, g2 = a
-            copy_on(eng, mg[:, it, g2], live[("M", it, g2)][:].rearrange("p t i -> p i t"))
-
-        def op_M1v(a, eng):
-            it = a[0]
+        def quantise_w(half, g):
+            cols = slice(BANK * half, BANK * half + BANK)
             nc.vector.quantize_mx(
-                out=m_codes[:, it].rearrange("p g i -> p (g i)").bitcast(FP8X4),
-                scales=m_sc[:, it].rearrange("p g i -> p (g i)"),
-                in_=mg[:, it].rearrange("p g i t -> p (g i t)"),
+                out=w_codes[:, g, cols].bitcast(FP8X4),
+                scales=w_scales[:, g, cols],
+                in_=w_grouped[:, g, cols, :].rearrange("p c t -> p (c t)"),
             )
 
-        def op_M2p(a, eng):
-            it, h = a
-            yp = psum.tile([P, 512], F32, name="yp", tag="ps")
-            cs = slice(512 * h, 512 * h + 512)
-            for g2 in range(2):
-                nc.tensor.matmul_mx(
-                    out=yp[:],
-                    lhsT=m_codes[:, it, g2, :].bitcast(FP8X4),
-                    lhsT_scale=m_sc[:, it, g2, :],
-                    rhs=w_codes[:, g2, cs].bitcast(FP8X4),
-                    rhs_scale=w_sc[:, g2, cs],
-                    start=(g2 == 0),
-                    stop=(g2 == 1),
+        def repeat_on_partitions(k):
+            bank = psum.tile([P, D], BF16, name="gb%d" % k, tag="gb%d" % k, bufs=1)
+            for half in range(2):
+                first = D * k + BANK * half
+                nc.tensor.matmul(
+                    out=bank[:, BANK * half : BANK * half + BANK],
+                    lhsT=ones[:],
+                    rhs=gb_row[:, first : first + BANK],
+                    start=True,
+                    stop=True,
                 )
-            live[("Y", it, h)] = yp
+            return bank
 
-        def op_S1(a, eng):
-            it, h = a
-            if h == 0:
-                live[("ysb", it)] = ypool.tile([P, D], F32, name="y_sb", tag="y_sb")
-                live[("sums", it)] = small.tile([P, 2], F32, name="sums", tag="sums")
-            cs = slice(512 * h, 512 * h + 512)
-            nc.scalar.activation(
-                out=live[("ysb", it)][:, cs], in_=live[("Y", it, h)][:], func=ACT.Copy, accum_out=live[("sums", it)][:, h : h + 1]
+        def first_matmul(t, g2):
+            bank = new_bank([P, PACK, P])
+            for t2 in range(PACK):
+                cols = slice((PACK * g2 + t2) * P, (PACK * g2 + t2 + 1) * P)
+                for g in range(PASSES):
+                    nc.tensor.matmul_mx(
+                        out=bank[:, t2, :],
+                        lhsT=feat_codes[:, g, cols].bitcast(FP8X4),
+                        lhsT_scale=feat_scales[:, g, cols],
+                        rhs=lap_codes[:, t, g, :].bitcast(FP8X4),
+                        rhs_scale=lap_scales[:, t, g, :],
+                        start=(g == 0),
+                        stop=(g == PASSES - 1),
+                    )
+            banks[("m", t, g2)] = bank
+
+        def copy_m(t, g2):
+            src = banks[("m", t, g2)][:].rearrange("p t i -> p i t")
+            if t in M_TILES_EMPTIED_BY_VECTOR:
+                nc.vector.tensor_copy(out=m_grouped[:, t, g2], in_=src)
+            else:
+                nc.scalar.copy(out=m_grouped[:, t, g2], in_=src)
+
+        def quantise_m(t):
+            nc.vector.quantize_mx(
+                out=m_codes[:, t].rearrange("p g i -> p (g i)").bitcast(FP8X4),
+                scales=m_scales[:, t].rearrange("p g i -> p (g i)"),
+                in_=m_grouped[:, t].rearrange("p g i t -> p (g i t)"),
             )
 
-        def op_NM(a, eng):
-            it = a[0]
-            negmu = small.tile([P, 1], F32, name="negmu", tag="negmu")
-            sums = live[("sums", it)]
+        def second_matmul(t, half):
+            bank = new_bank([P, BANK])
+            cols = slice(BANK * half, BANK * half + BANK)
+            for g2 in range(PASSES):
+                nc.tensor.matmul_mx(
+                    out=bank[:],
+                    lhsT=m_codes[:, t, g2, :].bitcast(FP8X4),
+                    lhsT_scale=m_scales[:, t, g2, :],
+                    rhs=w_codes[:, g2, cols].bitcast(FP8X4),
+                    rhs_scale=w_scales[:, g2, cols],
+                    start=(g2 == 0),
+                    stop=(g2 == PASSES - 1),
+                )
+            banks[("y", t, half)] = bank
+
+        def copy_y_and_sum(t, half):
+            if half == 0:
+                held[("y", t)] = rows.tile([P, D], F32, name="y_sb", tag="y_sb")
+                held[("sums", t)] = stats.tile([P, 2], F32, name="sums", tag="sums")
+            cols = slice(BANK * half, BANK * half + BANK)
+            nc.scalar.activation(
+                out=held[("y", t)][:, cols],
+                in_=banks[("y", t, half)][:],
+                func=ACT.Copy,
+                accum_out=held[("sums", t)][:, half : half + 1],
+            )
+
+        def minus_mean(t):
+            neg_mean = stats.tile([P, 1], F32, name="neg_mean", tag="neg_mean")
+            sums = held[("sums", t)]
             nc.vector.tensor_scalar(
-                out=negmu[:], in0=sums[:, 0:1], scalar1=sums[:, 1:2], scalar2=-1.0 / D, op0=ALU.add, op1=ALU.mult
+                out=neg_mean[:], in0=sums[:, 0:1], scalar1=sums[:, 1:2], scalar2=-1.0 / D, op0=ALU.add, op1=ALU.mult
             )
-            live[("negmu", it)] = negmu
+            held[("neg_mean", t)] = neg_mean
 
-        def op_S2(a, eng):
-            it = a[0]
-            ssq = small.tile([P, 1], F32, name="ssq", tag="ssq")
-            junk = keep.tile([P, D], BF16, name="junk", tag="junk")
+        def sum_of_squares(t):
+            ssq = stats.tile([P, 1], F32, name="ssq", tag="ssq")
             nc.scalar.activation(
-                out=junk[:], in_=live[("ysb", it)][:], func=ACT.Square, bias=live[("negmu", it)][:, 0:1], scale=1.0, accum_out=ssq[:]
+                out=squares[:],
+                in_=held[("y", t)][:],
+                func=ACT.Square,
+                bias=held[("neg_mean", t)][:, 0:1],
+                scale=1.0,
+                accum_out=ssq[:],
             )
-            live[("ssq", it)] = ssq
+            held[("ssq", t)] = ssq
 
-        def op_SQ(a, eng):
-            it = a[0]
-            rstd = small.tile([P, 1], F32, name="rstd", tag="rstd")
+        def inverse_std(t):
+            inv_std = stats.tile([P, 1], F32, name="inv_std", tag="inv_std")
             nc.scalar.activation(
-                out=rstd[:], in_=live[("ssq", it)][:], func=ACT.Abs_reciprocal_sqrt, bias=eps_t[:, 0:1], scale=1.0 / D
+                out=inv_std[:], in_=held[("ssq", t)][:], func=ACT.Abs_reciprocal_sqrt, bias=eps_col[:, 0:1], scale=1.0 / D
             )
-            live[("rstd", it)] = rstd
+            held[("inv_std", t)] = inv_std
 
-        def op_A(a, eng):
-            it = a[0]
-            z = opool.tile([P, D], F32, name="z", tag="z")
+        def centre_times_gamma(t):
+            z = rows.tile([P, D], F32, name="z", tag="z")
             nc.vector.scalar_tensor_tensor(
-                out=z[:], in0=live[("ysb", it)][:], scalar=live[("negmu", it)][:, 0:1], in1=live[("gb", 0)][:], op0=ALU.add, op1=ALU.mult
+                out=z[:], in0=held[("y", t)][:], scalar=held[("neg_mean", t)][:, 0:1], in1=gamma_bank[:], op0=ALU.add, op1=ALU.mult
             )
-            live[("z", it)] = z
+            held[("z", t)] = z
 
-        def op_B(a, eng):
-            it = a[0]
-            z = live[("z", it)]
+        def scale_plus_beta(t):
+            z = held[("z", t)]
             nc.vector.scalar_tensor_tensor(
-                out=z[:], in0=z[:], scalar=live[("rstd", it)][:, 0:1], in1=live[("gb", 1)][:], op0=ALU.mult, op1=ALU.add
+                out=z[:], in0=z[:], scalar=held[("inv_std", t)][:, 0:1], in1=beta_bank[:], op0=ALU.mult, op1=ALU.add
             )
 
-        def op_C(a, eng):
-            it = a[0]
-            z = live[("z", it)]
-            pieces = LAST_PIECES if it == LAST_TILE else 1
+        def leaky_and_store(t):
+            z = held[("z", t)]
+            pieces = LAST_STORES if t == TILES - 1 else 1
             width = D // pieces
             for c in range(pieces):
-                cs = slice(c * width, (c + 1) * width)
-                nc.vector.scalar_tensor_tensor(out=z[:, cs], in0=z[:, cs], scalar=SLOPE, in1=z[:, cs], op0=ALU.mult, op1=ALU.max)
-                nc.sync.dma_start(out=out_v[:, it, cs], in_=z[:, cs])
+                cols = slice(c * width, (c + 1) * width)
+                nc.vector.scalar_tensor_tensor(
+                    out=z[:, cols], in0=z[:, cols], scalar=SLOPE, in1=z[:, cols], op0=ALU.mult, op1=ALU.max
+                )
+                nc.sync.dma_start(out=out_rows[:, t, cols], in_=z[:, cols])
 
-        table = {
-            "GBp": op_GBp, "RG": op_RG, "FQ": op_FQ, "Lp": op_Lp, "Ls": op_Ls, "Lv": op_Lv, "Wp": op_Wp, "Ws": op_Ws,
-            "Wv": op_Wv, "M1p": op_M1p, "M1s": op_M1s, "M1v": op_M1v, "M2p": op_M2p, "S1": op_S1, "NM": op_NM,
-            "S2": op_S2, "SQ": op_SQ, "A": op_A, "B": op_B, "C": op_C,
-        }
-        for kind, args, eng in ORDER:
-            table[kind](args, eng)
+        for g in range(PASSES):
+            for block in range(4):
+                regroup_feat(g, block, on_vector=(block < 3))
+            for half in range(2):
+                quantise_feat(g, half)
+
+        def live(t):
+            return 0 <= t < TILES
+
+        for r in range(TILES + DEPTH):
+            if r == W_ROUND:
+                for pair in range(TILES // 2):
+                    for g in range(PASSES):
+                        transpose_w(pair, g)
+                    if pair == 0:
+                        gamma_bank = repeat_on_partitions(0)
+                        beta_bank = repeat_on_partitions(1)
+                    for g in range(PASSES):
+                        copy_w(pair, g)
+                    if pair % 2 == 1:
+                        for g in range(PASSES):
+                            quantise_w(pair // 2, g)
+            if live(r):
+                transpose_lap(r)
+            if live(r - 1):
+                for g2 in range(PASSES):
+                    first_matmul(r - 1, g2)
+            if live(r - 2):
+                for half in range(2):
+                    second_matmul(r - 2, half)
+            if live(r):
+                copy_lap(r)
+            if live(r - 1):
+                for g2 in range(PASSES):
+                    copy_m(r - 1, g2)
+            if live(r - 3):
+                sum_of_squares(r - 3)
+            if live(r - 2):
+                for half in range(2):
+                    copy_y_and_sum(r - 2, half)
+            if live(r - 3):
+                inverse_std(r - 3)
+            if live(r - 4):
+                scale_plus_beta(r - 4)
+            if live(r):
+                quantise_lap(r)
+            if live(r - 3):
+                centre_times_gamma(r - 3)
+            if live(r - 1):
+                quantise_m(r - 1)
+            if live(r - 4):
+                leaky_and_store(r - 4)
+            if live(r - 2):
+                minus_mean(r - 2)

from contextlib import ExitStack

import concourse.mybir as mybir
from concourse.masks import make_identity

F32 = mybir.dt.float32
BF16 = mybir.dt.bfloat16
U32 = mybir.dt.uint32
U8 = mybir.dt.uint8
FP8X4 = mybir.dt.float8_e4m3fn_x4
ALU = mybir.AluOpType
ACT = mybir.ActivationFunctionType

P = 128
N = 1024
D = 1024
TILES = N // P
PACK = 4
PASSES = 2
BANK = 512
EPS = 1e-5
SLOPE = 0.1
FLOPS = 2 * 2 * N * N * D

DEPTH = 4
W_ROUND = 1
M_TILES_EMPTIED_BY_VECTOR = (2, 3)
LAST_STORES = 2


def tile_gcn_pb_kernel(tc, lap, feat, w, gamma, beta, out):
    nc = tc.nc
    with ExitStack() as ctx:
        keep = ctx.enter_context(tc.tile_pool(name="keep", bufs=1))
        rows = ctx.enter_context(tc.tile_pool(name="rows", bufs=4))
        stats = ctx.enter_context(tc.tile_pool(name="stats", bufs=6))
        psum = ctx.enter_context(tc.psum_pool(name="psum", bufs=6))
        ctx.enter_context(tc.manual_schedule())

        gb_row = keep.tile([P, 2 * D], BF16)
        nc.vector.memset(gb_row[:], 0.0)
        nc.scalar.dma_start(out=gb_row[0:1, 0:D], in_=gamma.rearrange("(o d) -> o d", o=1))
        nc.scalar.dma_start(out=gb_row[0:1, D : 2 * D], in_=beta.rearrange("(o d) -> o d", o=1))
        eps_col = keep.tile([P, 1], F32)
        nc.vector.memset(eps_col[:], EPS)
        warm = keep.tile([P, 1], F32)
        nc.scalar.activation(out=warm[:], in_=eps_col[:], func=ACT.Abs_reciprocal_sqrt)
        ident = keep.tile([P, P], F32)
        make_identity(nc, ident[:])
        ones = keep.tile([P, P], BF16)
        nc.vector.memset(ones[:], 1.0)

        feat_raw = keep.tile([P, PASSES, PACK, D], BF16)
        lap_sb = keep.tile([P, TILES, N], BF16)
        w_sb = keep.tile([P, TILES, D], BF16)
        lap_rows = lap.rearrange("(p t) j -> p t j", t=TILES)

        def load_feat(g):
            for u in range(2):
                first = 512 * g + 256 * u
                nc.sync.dma_start(
                    out=feat_raw[:, g, 2 * u : 2 * u + 2, :],
                    in_=feat[first : first + 256, :].rearrange("(p e) d -> p e d", e=2),
                )

        def load_lap(t0, t1):
            nc.sync.dma_start(out=lap_sb[:, t0:t1, :], in_=lap_rows[:, t0:t1, :])

        load_feat(0)
        load_lap(0, 2)
        load_feat(1)
        for pair in range(TILES // 2):
            nc.sync.dma_start(
                out=w_sb[:, 2 * pair : 2 * pair + 2, :],
                in_=w[256 * pair : 256 * pair + 256, :].rearrange("(t p) d -> p t d", p=P),
            )
        load_lap(2, 4)
        load_lap(4, 8)
        lap_words = lap_sb[:].bitcast(F32)
        w_words = w_sb[:].bitcast(F32)

        feat_grouped = keep.tile([P, PASSES, D, PACK], BF16, align_bytes=64)
        feat_codes = keep.tile([P, PASSES, D], U32, align_bytes=64)
        feat_scales = keep.tile([P, PASSES, D], U8, align_bytes=64)
        lap_grouped = keep.tile([P, TILES, PASSES, P, PACK], BF16, align_bytes=64)
        lap_grouped_words = lap_grouped[:].bitcast(F32)
        lap_codes = keep.tile([P, TILES, PASSES, P], U32, align_bytes=64)
        lap_scales = keep.tile([P, TILES, PASSES, P], U8, align_bytes=64)
        w_grouped = keep.tile([P, PASSES, D, PACK], BF16, align_bytes=64)
        w_grouped_words = w_grouped[:].bitcast(F32)
        w_codes = keep.tile([P, PASSES, D], U32, align_bytes=64)
        w_scales = keep.tile([P, PASSES, D], U8, align_bytes=64)
        m_grouped = keep.tile([P, TILES, PASSES, P, PACK], BF16, align_bytes=64)
        m_codes = keep.tile([P, TILES, PASSES, P], U32, align_bytes=64)
        m_scales = keep.tile([P, TILES, PASSES, P], U8, align_bytes=64)
        squares = keep.tile([P, D], BF16)
        out_rows = out.rearrange("(p t) o -> p t o", t=TILES)
        banks = {}
        held = {}

        def new_bank(shape):
            return psum.tile(shape, F32, name="bank", tag="bank")

        def regroup_feat(g, block, on_vector):
            cols = slice(256 * block, 256 * block + 256)
            src = feat_raw[:, g, :, cols].rearrange("p t (c i e) -> p e c t i", i=4, e=2)
            dst = feat_grouped[:, g, cols, :].rearrange("p (e c i) t -> p e c t i", e=2, i=4)
            if on_vector:
                nc.vector.tensor_copy(out=dst, in_=src)
            else:
                for e in range(2):
                    nc.scalar.copy(out=dst[:, e], in_=src[:, e])

        def quantise_feat(g, half):
            cols = slice(BANK * half, BANK * half + BANK)
            nc.vector.quantize_mx(
                out=feat_codes[:, g, cols].bitcast(FP8X4),
                scales=feat_scales[:, g, cols],
                in_=feat_grouped[:, g, cols, :].rearrange("p c t -> p (c t)"),
            )

        def transpose_lap(t):
            bank = new_bank([P, PASSES, 2, P])
            for g in range(PASSES):
                for u in range(2):
                    first = 256 * g + 128 * u
                    nc.tensor.transpose(bank[:, g, u, :], lap_words[:, t, first : first + P], ident[:])
            banks[("lap", t)] = bank

        def copy_lap(t):
            nc.scalar.copy(out=lap_grouped_words[:, t], in_=banks[("lap", t)][:].rearrange("p g u i -> p g i u"))

        def quantise_lap(t):
            nc.vector.quantize_mx(
                out=lap_codes[:, t].rearrange("p g i -> p (g i)").bitcast(FP8X4),
                scales=lap_scales[:, t].rearrange("p g i -> p (g i)"),
                in_=lap_grouped[:, t].rearrange("p g i t -> p (g i t)"),
            )

        def transpose_w(pair, g):
            bank = new_bank([P, 2, 2, P])
            for b in range(2):
                for u in range(2):
                    first = 256 * g + 128 * u
                    nc.tensor.transpose(bank[:, u, b, :], w_words[:, 2 * pair + b, first : first + P], ident[:])
            banks[("w", pair, g)] = bank

        def copy_w(pair, g):
            nc.scalar.copy(
                out=w_grouped_words[:, g, 256 * pair : 256 * pair + 256, :],
                in_=banks[("w", pair, g)][:].rearrange("p u b o -> p (b o) u"),
            )

        def quantise_w(half, g):
            cols = slice(BANK * half, BANK * half + BANK)
            nc.vector.quantize_mx(
                out=w_codes[:, g, cols].bitcast(FP8X4),
                scales=w_scales[:, g, cols],
                in_=w_grouped[:, g, cols, :].rearrange("p c t -> p (c t)"),
            )

        def repeat_on_partitions(k):
            bank = psum.tile([P, D], BF16, name="gb%d" % k, tag="gb%d" % k, bufs=1)
            for half in range(2):
                first = D * k + BANK * half
                nc.tensor.matmul(
                    out=bank[:, BANK * half : BANK * half + BANK],
                    lhsT=ones[:],
                    rhs=gb_row[:, first : first + BANK],
                    start=True,
                    stop=True,
                )
            return bank

        def first_matmul(t, g2):
            bank = new_bank([P, PACK, P])
            for t2 in range(PACK):
                cols = slice((PACK * g2 + t2) * P, (PACK * g2 + t2 + 1) * P)
                for g in range(PASSES):
                    nc.tensor.matmul_mx(
                        out=bank[:, t2, :],
                        lhsT=feat_codes[:, g, cols].bitcast(FP8X4),
                        lhsT_scale=feat_scales[:, g, cols],
                        rhs=lap_codes[:, t, g, :].bitcast(FP8X4),
                        rhs_scale=lap_scales[:, t, g, :],
                        start=(g == 0),
                        stop=(g == PASSES - 1),
                    )
            banks[("m", t, g2)] = bank

        def copy_m(t, g2):
            src = banks[("m", t, g2)][:].rearrange("p t i -> p i t")
            if t in M_TILES_EMPTIED_BY_VECTOR:
                nc.vector.tensor_copy(out=m_grouped[:, t, g2], in_=src)
            else:
                nc.scalar.copy(out=m_grouped[:, t, g2], in_=src)

        def quantise_m(t):
            nc.vector.quantize_mx(
                out=m_codes[:, t].rearrange("p g i -> p (g i)").bitcast(FP8X4),
                scales=m_scales[:, t].rearrange("p g i -> p (g i)"),
                in_=m_grouped[:, t].rearrange("p g i t -> p (g i t)"),
            )

        def second_matmul(t, half):
            bank = new_bank([P, BANK])
            cols = slice(BANK * half, BANK * half + BANK)
            for g2 in range(PASSES):
                nc.tensor.matmul_mx(
                    out=bank[:],
                    lhsT=m_codes[:, t, g2, :].bitcast(FP8X4),
                    lhsT_scale=m_scales[:, t, g2, :],
                    rhs=w_codes[:, g2, cols].bitcast(FP8X4),
                    rhs_scale=w_scales[:, g2, cols],
                    start=(g2 == 0),
                    stop=(g2 == PASSES - 1),
                )
            banks[("y", t, half)] = bank

        def copy_y_and_sum(t, half):
            if half == 0:
                held[("y", t)] = rows.tile([P, D], F32, name="y_sb", tag="y_sb")
                held[("sums", t)] = stats.tile([P, 2], F32, name="sums", tag="sums")
            cols = slice(BANK * half, BANK * half + BANK)
            nc.scalar.activation(
                out=held[("y", t)][:, cols],
                in_=banks[("y", t, half)][:],
                func=ACT.Copy,
                accum_out=held[("sums", t)][:, half : half + 1],
            )

        def minus_mean(t):
            neg_mean = stats.tile([P, 1], F32, name="neg_mean", tag="neg_mean")
            sums = held[("sums", t)]
            nc.vector.tensor_scalar(
                out=neg_mean[:], in0=sums[:, 0:1], scalar1=sums[:, 1:2], scalar2=-1.0 / D, op0=ALU.add, op1=ALU.mult
            )
            held[("neg_mean", t)] = neg_mean

        def sum_of_squares(t):
            ssq = stats.tile([P, 1], F32, name="ssq", tag="ssq")
            nc.scalar.activation(
                out=squares[:],
                in_=held[("y", t)][:],
                func=ACT.Square,
                bias=held[("neg_mean", t)][:, 0:1],
                scale=1.0,
                accum_out=ssq[:],
            )
            held[("ssq", t)] = ssq

        def inverse_std(t):
            inv_std = stats.tile([P, 1], F32, name="inv_std", tag="inv_std")
            nc.scalar.activation(
                out=inv_std[:], in_=held[("ssq", t)][:], func=ACT.Abs_reciprocal_sqrt, bias=eps_col[:, 0:1], scale=1.0 / D
            )
            held[("inv_std", t)] = inv_std

        def centre_times_gamma(t):
            z = rows.tile([P, D], F32, name="z", tag="z")
            nc.vector.scalar_tensor_tensor(
                out=z[:], in0=held[("y", t)][:], scalar=held[("neg_mean", t)][:, 0:1], in1=gamma_bank[:], op0=ALU.add, op1=ALU.mult
            )
            held[("z", t)] = z

        def scale_plus_beta(t):
            z = held[("z", t)]
            nc.vector.scalar_tensor_tensor(
                out=z[:], in0=z[:], scalar=held[("inv_std", t)][:, 0:1], in1=beta_bank[:], op0=ALU.mult, op1=ALU.add
            )

        def leaky_and_store(t):
            z = held[("z", t)]
            pieces = LAST_STORES if t == TILES - 1 else 1
            width = D // pieces
            for c in range(pieces):
                cols = slice(c * width, (c + 1) * width)
                nc.vector.scalar_tensor_tensor(
                    out=z[:, cols], in0=z[:, cols], scalar=SLOPE, in1=z[:, cols], op0=ALU.mult, op1=ALU.max
                )
                nc.sync.dma_start(out=out_rows[:, t, cols], in_=z[:, cols])

        for g in range(PASSES):
            for block in range(4):
                regroup_feat(g, block, on_vector=(block < 3))
            for half in range(2):
                quantise_feat(g, half)

        def live(t):
            return 0 <= t < TILES

        for r in range(TILES + DEPTH):
            if r == W_ROUND:
                for pair in range(TILES // 2):
                    for g in range(PASSES):
                        transpose_w(pair, g)
                    if pair == 0:
                        gamma_bank = repeat_on_partitions(0)
                        beta_bank = repeat_on_partitions(1)
                    for g in range(PASSES):
                        copy_w(pair, g)
                    if pair % 2 == 1:
                        for g in range(PASSES):
                            quantise_w(pair // 2, g)
            if live(r):
                transpose_lap(r)
            if live(r - 1):
                for g2 in range(PASSES):
                    first_matmul(r - 1, g2)
            if live(r - 2):
                for half in range(2):
                    second_matmul(r - 2, half)
            if live(r):
                copy_lap(r)
            if live(r - 1):
                for g2 in range(PASSES):
                    copy_m(r - 1, g2)
            if live(r - 3):
                sum_of_squares(r - 3)
            if live(r - 2):
                for half in range(2):
                    copy_y_and_sum(r - 2, half)
            if live(r - 3):
                inverse_std(r - 3)
            if live(r - 4):
                scale_plus_beta(r - 4)
            if live(r):
                quantise_lap(r)
            if live(r - 3):
                centre_times_gamma(r - 3)
            if live(r - 1):
                quantise_m(r - 1)
            if live(r - 4):
                leaky_and_store(r - 4)
            if live(r - 2):
                minus_mean(r - 2)
